import numpy as np
import ml_dtypes


def mxq(x, axis, fmt="e4m3"):
    dtype, down = {"e4m3": (ml_dtypes.float8_e4m3fn, 7), "e5m2": (ml_dtypes.float8_e5m2, 14)}[fmt]
    v = np.moveaxis(np.asarray(x, np.float32).astype(ml_dtypes.bfloat16).astype(np.float64), axis, -1)
    blocks = v.reshape(v.shape[:-1] + (-1, 32))
    amax = np.abs(blocks).max(-1, keepdims=True)
    byte = np.maximum(np.where(amax > 0, np.frexp(amax)[1] - 1 + 127, 0) - down, 1)
    scale = np.exp2(byte - 127.0)
    codes = (blocks / scale).astype(np.float32).astype(dtype).astype(np.float64)
    return np.moveaxis((codes * scale).reshape(v.shape), -1, axis)


WIDE = False


def mx_kscale(k):
    if not WIDE:
        return np.ones(k)
    levels = np.array([10, -10, 5, -5, 0])
    a = np.random.permutation(np.resize(levels, k // 512 * 4)).reshape(k // 512, 4)
    idx = np.arange(k)
    return np.exp2(a[idx // 512, idx % 128 // 32])


BF16 = ml_dtypes.bfloat16


def bf(x):
    return np.asarray(x, np.float32).astype(BF16)


def f64(x):
    return np.asarray(x).astype(np.float64)


B, T, C, H, D, L = 1, 512, 2048, 16, 128, 512
THETA = 1.0e4


def rope(u, cos, sin):
    u0, u1 = u[..., 0::2], u[..., 1::2]
    c = cos[None, :, None, :]
    s = sin[None, :, None, :]
    o0 = u0 * c - u1 * s
    o1 = u0 * s + u1 * c
    return np.stack([o0, o1], axis=-1).reshape(u.shape)


def setup_inputs():
    s, t = mx_kscale(C), mx_kscale(L)
    inv_freq = 1.0 / (THETA ** (np.arange(0, D, 2) / D))
    ang = np.outer(np.arange(T), inv_freq)
    return {"x": bf(np.random.standard_normal((B, T, C)) * s),
            "freqs_cos": bf(np.cos(ang)),
            "freqs_sin": bf(np.sin(ang)),
            "wq": bf(np.random.standard_normal((H * D, C)) * 2.0 / np.sqrt(C) / s),
            "wkv_down": bf(np.random.standard_normal((L, C)) / np.sqrt(C) / s * t[:, None]),
            "wk_up": bf(np.random.standard_normal((D, L)) / np.sqrt(L) / t),
            "wv_up": bf(np.random.standard_normal((D, L)) / np.sqrt(L) / t)}


def reference(x, freqs_cos, freqs_sin, wq, wkv_down, wk_up, wv_up):
    cos, sin = f64(freqs_cos), f64(freqs_sin)
    xq = mxq(f64(x), 2, "e4m3")
    q = (xq @ mxq(f64(wq), 1, "e4m3").T).reshape(B, T, H, D)
    kv_latent = xq @ mxq(f64(wkv_down), 1, "e4m3").T
    lq = mxq(kv_latent, 2, "e4m3")
    k = lq @ mxq(f64(wk_up), 1, "e4m3").T
    v = lq @ mxq(f64(wv_up), 1, "e4m3").T
    q_rot = rope(q, cos, sin)
    k_rot = rope(k[:, :, None, :], cos, sin)[:, :, 0, :]
    return q_rot, k_rot, v

@@ -1,0 +1,240 @@
+from contextlib import ExitStack
+
+import concourse.mybir as mybir
+from concourse.masks import make_identity
+
+F32 = mybir.dt.float32
+BF16 = mybir.dt.bfloat16
+U32 = mybir.dt.uint32
+U8 = mybir.dt.uint8
+FP8X4 = mybir.dt.float8_e4m3fn_x4
+MULT = mybir.AluOpType.mult
+ADD = mybir.AluOpType.add
+
+P = 128
+TOKENS = 512
+CHANNELS = 2048
+HEADS = 16
+HEAD_DIM = 128
+LATENT = 512
+PAIRS = HEAD_DIM // 2
+K_PASS = 512
+PASSES = CHANNELS // K_PASS
+TOKEN_BLOCKS = TOKENS // P
+LATENT_BLOCKS = LATENT // P
+GROUP_HEADS = 4
+GROUPS = HEADS // GROUP_HEADS
+GROUP_COLS = GROUP_HEADS * HEAD_DIM
+HEADS_PER_RUN = 2
+BLOCKS_PER_RUN = 2
+RUNS = HEADS // HEADS_PER_RUN
+
+FLOPS = 2 * TOKENS * CHANNELS * (HEADS * HEAD_DIM + LATENT) + 2 * TOKENS * LATENT * 2 * HEAD_DIM
+
+
+def tile_attention_pa_kernel(
+    tc, x, freqs_cos, freqs_sin, wq, wkv_down, wk_up, wv_up, out_0, out_1, out_2
+):
+    nc = tc.nc
+    with ExitStack() as ctx:
+        keep = ctx.enter_context(tc.tile_pool(name="keep", bufs=1))
+        grouped_pool = ctx.enter_context(tc.tile_pool(name="grouped", bufs=4))
+        wq_code_pool = ctx.enter_context(tc.tile_pool(name="wq_code", bufs=2))
+        product_pool = ctx.enter_context(tc.tile_pool(name="product", bufs=3))
+        rotated_pool = ctx.enter_context(tc.tile_pool(name="rotated", bufs=4))
+        flip_psum = ctx.enter_context(tc.psum_pool(name="flip", bufs=4))
+        sum_psum = ctx.enter_context(tc.psum_pool(name="sums", bufs=4))
+        ctx.enter_context(tc.manual_schedule())
+
+        x_blocks = x.flatten_outer_dims().rearrange("(p i) c -> i p c", i=TOKEN_BLOCKS)
+        cos_view = freqs_cos.rearrange("(p i) j -> p i j", i=TOKEN_BLOCKS)
+        sin_view = freqs_sin.rearrange("(p i) j -> p i j", i=TOKEN_BLOCKS)
+        q_blocks = out_0.flatten_outer_dims().rearrange(
+            "(p i h) d -> i p h d", i=TOKEN_BLOCKS, h=HEADS
+        )
+        k_view = out_1.flatten_outer_dims().rearrange("(p i) d -> p i d", i=TOKEN_BLOCKS)
+        v_view = out_2.flatten_outer_dims().rearrange("(p i) d -> p i d", i=TOKEN_BLOCKS)
+        wkv_blocks = wkv_down.rearrange("(u p e) c -> u e p c", u=2, e=2)
+        wq_runs = wq.rearrange("(n a p) c -> n p a c", a=HEADS_PER_RUN, p=P)
+
+        x_raw = []
+        for i in range(TOKEN_BLOCKS):
+            x_raw.append(keep.tile([P, CHANNELS], BF16, name="x_raw%d" % i))
+            nc.sync.dma_start(out=x_raw[i][:], in_=x_blocks[i])
+        wkv_raw = []
+        for t in range(LATENT_BLOCKS):
+            wkv_raw.append(keep.tile([P, CHANNELS], BF16, name="wkv_raw%d" % t))
+            nc.sync.dma_start(out=wkv_raw[t][:], in_=wkv_blocks[t // 2, t % 2])
+        wq_raw = []
+        for run in range(RUNS):
+            wq_raw.append(keep.tile([P, HEADS_PER_RUN, CHANNELS], BF16, name="wq_raw%d" % run))
+            nc.sync.dma_start(out=wq_raw[run][:], in_=wq_runs[run])
+        rotary = keep.tile([P, TOKEN_BLOCKS, 2, 2, PAIRS], BF16)
+        nc.scalar.dma_start(out=rotary[:, :, 0, 0, :], in_=cos_view)
+        nc.scalar.dma_start(out=rotary[:, :, 1, 0, :], in_=sin_view)
+        nc.scalar.dma_start(out=rotary[:, :, 1, 1, :], in_=cos_view)
+        up_raw = []
+        for s, weight in enumerate((wk_up, wv_up)):
+            up_raw.append(keep.tile([P, LATENT], BF16, name="up_raw%d" % s))
+            nc.scalar.dma_start(out=up_raw[s][:], in_=weight)
+
+        identity = keep.tile([P, P], F32)
+        make_identity(nc, identity[:])
+
+        x_codes = keep.tile([P, PASSES, TOKENS], U32, align_bytes=64)
+        x_scales = keep.tile([P, PASSES, TOKENS], U8, align_bytes=64)
+        wkv_codes = keep.tile([P, PASSES, LATENT], U32, align_bytes=64)
+        wkv_scales = keep.tile([P, PASSES, LATENT], U8, align_bytes=64)
+        up_codes = keep.tile([P, 2 * HEAD_DIM], U32, align_bytes=64)
+        up_scales = keep.tile([P, 2 * HEAD_DIM], U8, align_bytes=64)
+        latent_codes = keep.tile([P, TOKENS], U32, align_bytes=64)
+        latent_scales = keep.tile([P, TOKENS], U8, align_bytes=64)
+        wq_codes = {}
+        wq_scales = {}
+
+        def flip_bank(slabs, grouped_words):
+            bank = flip_psum.tile([P, 2, 2, P], F32, name="bank")
+            for s in range(2):
+                for u in range(2):
+                    nc.tensor.transpose(bank[:, s, u, :], slabs[s][:, u * P : (u + 1) * P], identity[:])
+            nc.scalar.copy(out=grouped_words, in_=bank[:].rearrange("p s u r -> p s r u"))
+
+        def quantise(grouped, codes, scales):
+            nc.vector.quantize_mx(out=codes.bitcast(FP8X4), scales=scales, in_=grouped)
+
+        def flip_and_quantise(raw, codes, scales, first_row):
+            words = raw.bitcast(F32)
+            grouped = grouped_pool.tile([P, PASSES * P * 4], BF16, name="grouped", align_bytes=64)
+            grouped_words = grouped[:].bitcast(F32).rearrange(
+                "p (b s r u) -> p b s r u", b=PASSES // 2, s=2, u=2
+            )
+            for b in range(PASSES // 2):
+                slabs = [words[:, (2 * b + s) * 2 * P : (2 * b + s + 1) * 2 * P] for s in range(2)]
+                flip_bank(slabs, grouped_words[:, b])
+            rows = slice(first_row, first_row + P)
+            for g in range(PASSES):
+                quantise(grouped[:, g * 4 * P : (g + 1) * 4 * P], codes[:, g, rows], scales[:, g, rows])
+
+        def flip_heads(run):
+            for a in range(HEADS_PER_RUN):
+                group, member = divmod(run * HEADS_PER_RUN + a, GROUP_HEADS)
+                if member == 0:
+                    wq_codes[group] = wq_code_pool.tile(
+                        [P, PASSES, GROUP_COLS], U32, name="wq_codes", align_bytes=64
+                    )
+                    wq_scales[group] = wq_code_pool.tile(
+                        [P, PASSES, GROUP_COLS], U8, name="wq_scales", align_bytes=64
+                    )
+                flip_and_quantise(wq_raw[run][:, a, :], wq_codes[group], wq_scales[group], member * P)
+
+        def rotate(sums, heads, i, rotated):
+            shape = [P, 2, 2, heads, PAIRS]
+            product = product_pool.tile(shape, F32, name="product")
+            nc.vector.tensor_tensor(
+                out=product[:],
+                in0=sums.rearrange("p (h j e) -> p e h j", h=heads, e=2).unsqueeze(1).to_broadcast(shape),
+                in1=rotary[:, i].unsqueeze(3).to_broadcast(shape),
+                op=MULT,
+            )
+            nc.gpsimd.tensor_tensor(
+                out=rotated.rearrange("p (h j o) -> p h j o", h=heads, o=2),
+                in0=product[:, :, 0].rearrange("p o h j -> p h j o"),
+                in1=product[:, :, 1].rearrange("p o h j -> p h j o"),
+                op=ADD,
+            )
+
+        def q_passes(run):
+            group, half = divmod(run, TOKEN_BLOCKS // BLOCKS_PER_RUN)
+            for i in range(half * BLOCKS_PER_RUN, (half + 1) * BLOCKS_PER_RUN):
+                tokens = slice(i * P, (i + 1) * P)
+                q_sums = sum_psum.tile([P, GROUP_COLS], F32, name="q_sums", tag="sums")
+                for g in range(PASSES):
+                    nc.tensor.matmul_mx(
+                        out=q_sums[:],
+                        lhsT=x_codes[:, g, tokens].bitcast(FP8X4),
+                        lhsT_scale=x_scales[:, g, tokens],
+                        rhs=wq_codes[group][:, g, :].bitcast(FP8X4),
+                        rhs_scale=wq_scales[group][:, g, :],
+                        start=(g == 0),
+                        stop=(g == PASSES - 1),
+                    )
+                q_rotated = rotated_pool.tile([P, GROUP_COLS], F32, name="q_rotated")
+                rotate(q_sums[:], GROUP_HEADS, i, q_rotated[:])
+                nc.sync.dma_start(
+                    out=q_blocks[i][:, group * GROUP_HEADS : (group + 1) * GROUP_HEADS, :],
+                    in_=q_rotated[:].rearrange("p (h d) -> p h d", h=GROUP_HEADS),
+                )
+
+        def latent_passes(t):
+            channels = slice(t * P, (t + 1) * P)
+            for i in range(TOKEN_BLOCKS):
+                tokens = slice(i * P, (i + 1) * P)
+                for g in range(PASSES):
+                    nc.tensor.matmul_mx(
+                        out=latent_sums[i][:, t, :],
+                        lhsT=wkv_codes[:, g, channels].bitcast(FP8X4),
+                        lhsT_scale=wkv_scales[:, g, channels],
+                        rhs=x_codes[:, g, tokens].bitcast(FP8X4),
+                        rhs_scale=x_scales[:, g, tokens],
+                        start=(g == 0),
+                        stop=(g == PASSES - 1),
+                    )
+
+        for i in range(TOKEN_BLOCKS):
+            flip_and_quantise(x_raw[i][:], x_codes, x_scales, i * P)
+        nc.vector.tensor_scalar_mul(out=rotary[:, :, 0, 1, :], in0=rotary[:, :, 1, 0, :], scalar1=-1.0)
+
+        latent_sums = [
+            sum_psum.tile([P, LATENT_BLOCKS, P], F32, name="latent_sums%d" % i, tag="sums")
+            for i in range(TOKEN_BLOCKS)
+        ]
+        flip_and_quantise(wkv_raw[0][:], wkv_codes, wkv_scales, 0)
+        for t in range(1, LATENT_BLOCKS):
+            flip_and_quantise(wkv_raw[t][:], wkv_codes, wkv_scales, t * P)
+            latent_passes(t - 1)
+
+        up_grouped = keep.tile([P, 2 * HEAD_DIM * 4], BF16, align_bytes=64)
+        flip_bank(
+            [up_raw[s][:].bitcast(F32) for s in range(2)],
+            up_grouped[:].bitcast(F32).rearrange("p (s r u) -> p s r u", s=2, u=2),
+        )
+        quantise(up_grouped[:], up_codes[:], up_scales[:])
+        flip_heads(0)
+        latent_passes(LATENT_BLOCKS - 1)
+
+        latent_grouped = keep.tile([P, TOKENS * 4], BF16, align_bytes=64)
+        latent_view = latent_grouped[:].rearrange("p (i r t) -> p i r t", i=TOKEN_BLOCKS, t=LATENT_BLOCKS)
+        for i in range(TOKEN_BLOCKS):
+            nc.vector.tensor_copy(out=latent_view[:, i], in_=latent_sums[i][:].rearrange("p t r -> p r t"))
+        quantise(latent_grouped[:], latent_codes[:], latent_scales[:])
+
+        flip_heads(1)
+        flip_heads(2)
+
+        k_rotated = keep.tile([P, TOKEN_BLOCKS, HEAD_DIM], F32)
+        v_copied = keep.tile([P, TOKEN_BLOCKS, HEAD_DIM], F32)
+        for b in range(TOKEN_BLOCKS // 2):
+            kv_sums = sum_psum.tile([P, 2, 2 * HEAD_DIM], F32, name="kv_sums", tag="sums")
+            for s in range(2):
+                tokens = slice((2 * b + s) * P, (2 * b + s + 1) * P)
+                nc.tensor.matmul_mx(
+                    out=kv_sums[:, s, :],
+                    lhsT=latent_codes[:, tokens].bitcast(FP8X4),
+                    lhsT_scale=latent_scales[:, tokens],
+                    rhs=up_codes[:].bitcast(FP8X4),
+                    rhs_scale=up_scales[:],
+                    start=True,
+                    stop=True,
+                )
+            for s in range(2):
+                rotate(kv_sums[:, s, 0:HEAD_DIM], 1, 2 * b + s, k_rotated[:, 2 * b + s, :])
+            nc.vector.tensor_copy(out=v_copied[:, 2 * b : 2 * b + 2, :], in_=kv_sums[:, :, HEAD_DIM : 2 * HEAD_DIM])
+        nc.sync.dma_start(out=k_view, in_=k_rotated[:])
+        nc.sync.dma_start(out=v_view, in_=v_copied[:])
+
+        q_passes(0)
+        for run in range(3, RUNS):
+            flip_heads(run)
+            q_passes(run - 2)
+        q_passes(RUNS - 2)
+        q_passes(RUNS - 1)

@@ -114,6 +114,7 @@ def tile_attention_pa_kernel(
             rows = slice(first_row, first_row + P)
             for g in range(PASSES):
                 quantise(grouped[:, g * 4 * P : (g + 1) * 4 * P], codes[:, g, rows], scales[:, g, rows])
+                finish_deferred()
 
         def flip_heads(run):
             for a in range(HEADS_PER_RUN):
@@ -136,12 +137,18 @@ def tile_attention_pa_kernel(
                 in1=rotary[:, i].unsqueeze(3).to_broadcast(shape),
                 op=MULT,
             )
-            nc.gpsimd.tensor_tensor(
-                out=rotated.rearrange("p (h j o) -> p h j o", h=heads, o=2),
-                in0=product[:, :, 0].rearrange("p o h j -> p h j o"),
-                in1=product[:, :, 1].rearrange("p o h j -> p h j o"),
-                op=ADD,
-            )
+
+            def add(engine):
+                engine.tensor_tensor(
+                    out=rotated.rearrange("p (h j o) -> p h j o", h=heads, o=2),
+                    in0=product[:, :, 0].rearrange("p o h j -> p h j o"),
+                    in1=product[:, :, 1].rearrange("p o h j -> p h j o"),
+                    op=ADD,
+                )
+
+            return add
+
+        deferred = []
 
         def q_passes(run):
             group, half = divmod(run, TOKEN_BLOCKS // BLOCKS_PER_RUN)
@@ -159,11 +166,23 @@ def tile_attention_pa_kernel(
                         stop=(g == PASSES - 1),
                     )
                 q_rotated = rotated_pool.tile([P, GROUP_COLS], F32, name="q_rotated")
-                rotate(q_sums[:], GROUP_HEADS, i, q_rotated[:])
-                nc.sync.dma_start(
-                    out=q_blocks[i][:, group * GROUP_HEADS : (group + 1) * GROUP_HEADS, :],
-                    in_=q_rotated[:].rearrange("p (h d) -> p h d", h=GROUP_HEADS),
-                )
+                add = rotate(q_sums[:], GROUP_HEADS, i, q_rotated[:])
+
+                def finish(engine, add=add, i=i, q_rotated=q_rotated):
+                    add(engine)
+                    nc.sync.dma_start(
+                        out=q_blocks[i][:, group * GROUP_HEADS : (group + 1) * GROUP_HEADS, :],
+                        in_=q_rotated[:].rearrange("p (h d) -> p h d", h=GROUP_HEADS),
+                    )
+
+                if i % BLOCKS_PER_RUN == 0:
+                    finish(nc.gpsimd)
+                else:
+                    deferred.append(finish)
+
+        def finish_deferred():
+            while deferred:
+                deferred.pop()(nc.vector)
 
         def latent_passes(t):
             channels = slice(t * P, (t + 1) * P)
@@ -227,7 +246,7 @@ def tile_attention_pa_kernel(
                     stop=True,
                 )
             for s in range(2):
-                rotate(kv_sums[:, s, 0:HEAD_DIM], 1, 2 * b + s, k_rotated[:, 2 * b + s, :])
+                rotate(kv_sums[:, s, 0:HEAD_DIM], 1, 2 * b + s, k_rotated[:, 2 * b + s, :])(nc.gpsimd)
             nc.vector.tensor_copy(out=v_copied[:, 2 * b : 2 * b + 2, :], in_=kv_sums[:, :, HEAD_DIM : 2 * HEAD_DIM])
         nc.sync.dma_start(out=k_view, in_=k_rotated[:])
         nc.sync.dma_start(out=v_view, in_=v_copied[:])
@@ -237,4 +256,6 @@ def tile_attention_pa_kernel(
             flip_heads(run)
             q_passes(run - 2)
         q_passes(RUNS - 2)
+        finish_deferred()
         q_passes(RUNS - 1)
+        finish_deferred()

@@ -81,10 +81,10 @@ def tile_attention_pa_kernel(
         identity = keep.tile([P, P], F32)
         make_identity(nc, identity[:])
 
-        x_codes = keep.tile([P, PASSES, TOKENS], U32, align_bytes=64)
-        x_scales = keep.tile([P, PASSES, TOKENS], U8, align_bytes=64)
-        wkv_codes = keep.tile([P, PASSES, LATENT], U32, align_bytes=64)
-        wkv_scales = keep.tile([P, PASSES, LATENT], U8, align_bytes=64)
+        x_codes = keep.tile([P, TOKEN_BLOCKS, PASSES, P], U32, align_bytes=64)
+        x_scales = keep.tile([P, TOKEN_BLOCKS, PASSES, P], U8, align_bytes=64)
+        wkv_codes = keep.tile([P, LATENT_BLOCKS, PASSES, P], U32, align_bytes=64)
+        wkv_scales = keep.tile([P, LATENT_BLOCKS, PASSES, P], U8, align_bytes=64)
         up_codes = keep.tile([P, 2 * HEAD_DIM], U32, align_bytes=64)
         up_scales = keep.tile([P, 2 * HEAD_DIM], U8, align_bytes=64)
         latent_codes = keep.tile([P, TOKENS], U32, align_bytes=64)
@@ -102,47 +102,63 @@ def tile_attention_pa_kernel(
         def quantise(grouped, codes, scales):
             nc.vector.quantize_mx(out=codes.bitcast(FP8X4), scales=scales, in_=grouped)
 
-        def flip_and_quantise(raw, codes, scales, first_row):
+        def flip_block(raw, codes, scales):
             words = raw.bitcast(F32)
-            grouped = grouped_pool.tile([P, PASSES * P * 4], BF16, name="grouped", align_bytes=64)
-            grouped_words = grouped[:].bitcast(F32).rearrange(
-                "p (b s r u) -> p b s r u", b=PASSES // 2, s=2, u=2
-            )
+            grouped = grouped_pool.tile([P, PASSES, P * 4], BF16, name="grouped", align_bytes=64)
             for b in range(PASSES // 2):
-                slabs = [words[:, (2 * b + s) * 2 * P : (2 * b + s + 1) * 2 * P] for s in range(2)]
-                flip_bank(slabs, grouped_words[:, b])
-            rows = slice(first_row, first_row + P)
-            for g in range(PASSES):
-                quantise(grouped[:, g * 4 * P : (g + 1) * 4 * P], codes[:, g, rows], scales[:, g, rows])
-                finish_deferred()
+                passes = slice(2 * b, 2 * b + 2)
+                flip_bank(
+                    [words[:, g * 2 * P : (g + 1) * 2 * P] for g in (2 * b, 2 * b + 1)],
+                    grouped[:, passes].rearrange("p s w -> p (s w)").bitcast(F32).rearrange(
+                        "p (s r u) -> p s r u", s=2, u=2
+                    ),
+                )
+            for b in range(PASSES // 2):
+                passes = slice(2 * b, 2 * b + 2)
+                quantise(
+                    grouped[:, passes].rearrange("p s w -> p (s w)"),
+                    codes[:, passes].rearrange("p s r -> p (s r)"),
+                    scales[:, passes].rearrange("p s r -> p (s r)"),
+                )
 
         def flip_heads(run):
-            for a in range(HEADS_PER_RUN):
-                group, member = divmod(run * HEADS_PER_RUN + a, GROUP_HEADS)
-                if member == 0:
-                    wq_codes[group] = wq_code_pool.tile(
-                        [P, PASSES, GROUP_COLS], U32, name="wq_codes", align_bytes=64
-                    )
-                    wq_scales[group] = wq_code_pool.tile(
-                        [P, PASSES, GROUP_COLS], U8, name="wq_scales", align_bytes=64
-                    )
-                flip_and_quantise(wq_raw[run][:, a, :], wq_codes[group], wq_scales[group], member * P)
+            group, half = divmod(run, GROUP_HEADS // HEADS_PER_RUN)
+            if half == 0:
+                wq_codes[group] = wq_code_pool.tile(
+                    [P, PASSES, GROUP_COLS], U32, name="wq_codes", align_bytes=64
+                )
+                wq_scales[group] = wq_code_pool.tile(
+                    [P, PASSES, GROUP_COLS], U8, name="wq_scales", align_bytes=64
+                )
+            run_cols = HEADS_PER_RUN * HEAD_DIM
+            cols = slice(half * run_cols, (half + 1) * run_cols)
+            words = [wq_raw[run][:, a, :].bitcast(F32) for a in range(HEADS_PER_RUN)]
+            grouped = grouped_pool.tile([P, PASSES, run_cols * 4], BF16, name="grouped_heads", align_bytes=64)
+            for g in range(PASSES):
+                flip_bank(
+                    [w[:, g * 2 * P : (g + 1) * 2 * P] for w in words],
+                    grouped[:, g].bitcast(F32).rearrange("p (s r u) -> p s r u", s=2, u=2),
+                )
+            for g in range(PASSES):
+                quantise(grouped[:, g], wq_codes[group][:, g, cols], wq_scales[group][:, g, cols])
+                finish_deferred()
 
-        def rotate(sums, heads, i, rotated):
-            shape = [P, 2, 2, heads, PAIRS]
-            product = product_pool.tile(shape, F32, name="product")
+        def rotate(sums, table, rotated):
+            count = sums.shape[1]
+            shape = [P, 2, 2, count, PAIRS]
+            product = product_pool.tile(shape, F32, name="product", tag="product%d" % count)
             nc.vector.tensor_tensor(
                 out=product[:],
-                in0=sums.rearrange("p (h j e) -> p e h j", h=heads, e=2).unsqueeze(1).to_broadcast(shape),
-                in1=rotary[:, i].unsqueeze(3).to_broadcast(shape),
+                in0=sums.rearrange("p n (j e) -> p e n j", e=2).unsqueeze(1).to_broadcast(shape),
+                in1=table.to_broadcast(shape),
                 op=MULT,
             )
 
             def add(engine):
                 engine.tensor_tensor(
-                    out=rotated.rearrange("p (h j o) -> p h j o", h=heads, o=2),
-                    in0=product[:, :, 0].rearrange("p o h j -> p h j o"),
-                    in1=product[:, :, 1].rearrange("p o h j -> p h j o"),
+                    out=rotated.rearrange("p n (j o) -> p n j o", o=2),
+                    in0=product[:, :, 0].rearrange("p o n j -> p n j o"),
+                    in1=product[:, :, 1].rearrange("p o n j -> p n j o"),
                     op=ADD,
                 )
 
@@ -153,26 +169,27 @@ def tile_attention_pa_kernel(
         def q_passes(run):
             group, half = divmod(run, TOKEN_BLOCKS // BLOCKS_PER_RUN)
             for i in range(half * BLOCKS_PER_RUN, (half + 1) * BLOCKS_PER_RUN):
-                tokens = slice(i * P, (i + 1) * P)
                 q_sums = sum_psum.tile([P, GROUP_COLS], F32, name="q_sums", tag="sums")
                 for g in range(PASSES):
                     nc.tensor.matmul_mx(
                         out=q_sums[:],
-                        lhsT=x_codes[:, g, tokens].bitcast(FP8X4),
-                        lhsT_scale=x_scales[:, g, tokens],
+                        lhsT=x_codes[:, i, g, :].bitcast(FP8X4),
+                        lhsT_scale=x_scales[:, i, g, :],
                         rhs=wq_codes[group][:, g, :].bitcast(FP8X4),
                         rhs_scale=wq_scales[group][:, g, :],
                         start=(g == 0),
                         stop=(g == PASSES - 1),
                     )
-                q_rotated = rotated_pool.tile([P, GROUP_COLS], F32, name="q_rotated")
-                add = rotate(q_sums[:], GROUP_HEADS, i, q_rotated[:])
+                q_rotated = rotated_pool.tile([P, GROUP_HEADS, HEAD_DIM], F32, name="q_rotated")
+                add = rotate(
+                    q_sums[:].rearrange("p (h d) -> p h d", h=GROUP_HEADS), rotary[:, i].unsqueeze(3), q_rotated[:]
+                )
 
                 def finish(engine, add=add, i=i, q_rotated=q_rotated):
                     add(engine)
                     nc.sync.dma_start(
                         out=q_blocks[i][:, group * GROUP_HEADS : (group + 1) * GROUP_HEADS, :],
-                        in_=q_rotated[:].rearrange("p (h d) -> p h d", h=GROUP_HEADS),
+                        in_=q_rotated[:],
                     )
 
                 if i % BLOCKS_PER_RUN == 0:
@@ -185,31 +202,29 @@ def tile_attention_pa_kernel(
                 deferred.pop()(nc.vector)
 
         def latent_passes(t):
-            channels = slice(t * P, (t + 1) * P)
             for i in range(TOKEN_BLOCKS):
-                tokens = slice(i * P, (i + 1) * P)
                 for g in range(PASSES):
                     nc.tensor.matmul_mx(
                         out=latent_sums[i][:, t, :],
-                        lhsT=wkv_codes[:, g, channels].bitcast(FP8X4),
-                        lhsT_scale=wkv_scales[:, g, channels],
-                        rhs=x_codes[:, g, tokens].bitcast(FP8X4),
-                        rhs_scale=x_scales[:, g, tokens],
+                        lhsT=wkv_codes[:, t, g, :].bitcast(FP8X4),
+                        lhsT_scale=wkv_scales[:, t, g, :],
+                        rhs=x_codes[:, i, g, :].bitcast(FP8X4),
+                        rhs_scale=x_scales[:, i, g, :],
                         start=(g == 0),
                         stop=(g == PASSES - 1),
                     )
 
         for i in range(TOKEN_BLOCKS):
-            flip_and_quantise(x_raw[i][:], x_codes, x_scales, i * P)
+            flip_block(x_raw[i][:], x_codes[:, i], x_scales[:, i])
         nc.vector.tensor_scalar_mul(out=rotary[:, :, 0, 1, :], in0=rotary[:, :, 1, 0, :], scalar1=-1.0)
 
         latent_sums = [
             sum_psum.tile([P, LATENT_BLOCKS, P], F32, name="latent_sums%d" % i, tag="sums")
             for i in range(TOKEN_BLOCKS)
         ]
-        flip_and_quantise(wkv_raw[0][:], wkv_codes, wkv_scales, 0)
+        flip_block(wkv_raw[0][:], wkv_codes[:, 0], wkv_scales[:, 0])
         for t in range(1, LATENT_BLOCKS):
-            flip_and_quantise(wkv_raw[t][:], wkv_codes, wkv_scales, t * P)
+            flip_block(wkv_raw[t][:], wkv_codes[:, t], wkv_scales[:, t])
             latent_passes(t - 1)
 
         up_grouped = keep.tile([P, 2 * HEAD_DIM * 4], BF16, align_bytes=64)
@@ -224,7 +239,7 @@ def tile_attention_pa_kernel(
         latent_grouped = keep.tile([P, TOKENS * 4], BF16, align_bytes=64)
         latent_view = latent_grouped[:].rearrange("p (i r t) -> p i r t", i=TOKEN_BLOCKS, t=LATENT_BLOCKS)
         for i in range(TOKEN_BLOCKS):
-            nc.vector.tensor_copy(out=latent_view[:, i], in_=latent_sums[i][:].rearrange("p t r -> p r t"))
+            nc.scalar.copy(out=latent_view[:, i], in_=latent_sums[i][:].rearrange("p t r -> p r t"))
         quantise(latent_grouped[:], latent_codes[:], latent_scales[:])
 
         flip_heads(1)
@@ -233,21 +248,25 @@ def tile_attention_pa_kernel(
         k_rotated = keep.tile([P, TOKEN_BLOCKS, HEAD_DIM], F32)
         v_copied = keep.tile([P, TOKEN_BLOCKS, HEAD_DIM], F32)
         for b in range(TOKEN_BLOCKS // 2):
-            kv_sums = sum_psum.tile([P, 2, 2 * HEAD_DIM], F32, name="kv_sums", tag="sums")
-            for s in range(2):
-                tokens = slice((2 * b + s) * P, (2 * b + s + 1) * P)
-                nc.tensor.matmul_mx(
-                    out=kv_sums[:, s, :],
-                    lhsT=latent_codes[:, tokens].bitcast(FP8X4),
-                    lhsT_scale=latent_scales[:, tokens],
-                    rhs=up_codes[:].bitcast(FP8X4),
-                    rhs_scale=up_scales[:],
-                    start=True,
-                    stop=True,
-                )
-            for s in range(2):
-                rotate(kv_sums[:, s, 0:HEAD_DIM], 1, 2 * b + s, k_rotated[:, 2 * b + s, :])(nc.gpsimd)
-            nc.vector.tensor_copy(out=v_copied[:, 2 * b : 2 * b + 2, :], in_=kv_sums[:, :, HEAD_DIM : 2 * HEAD_DIM])
+            kv_sums = sum_psum.tile([P, 2, 2, HEAD_DIM], F32, name="kv_sums", tag="sums")
+            for w in range(2):
+                cols = slice(w * HEAD_DIM, (w + 1) * HEAD_DIM)
+                for s in range(2):
+                    tokens = slice((2 * b + s) * P, (2 * b + s + 1) * P)
+                    nc.tensor.matmul_mx(
+                        out=kv_sums[:, w, s, :],
+                        lhsT=latent_codes[:, tokens].bitcast(FP8X4),
+                        lhsT_scale=latent_scales[:, tokens],
+                        rhs=up_codes[:, cols].bitcast(FP8X4),
+                        rhs_scale=up_scales[:, cols],
+                        start=True,
+                        stop=True,
+                    )
+            blocks = slice(2 * b, 2 * b + 2)
+            rotate(
+                kv_sums[:, 0], rotary[:, blocks].rearrange("p n o e j -> p o e n j"), k_rotated[:, blocks, :]
+            )(nc.gpsimd)
+            nc.scalar.copy(out=v_copied[:, 2 * b : 2 * b + 2, :], in_=kv_sums[:, 1])
         nc.sync.dma_start(out=k_view, in_=k_rotated[:])
         nc.sync.dma_start(out=v_view, in_=v_copied[:])
 

@@ -57,18 +57,34 @@ def tile_attention_pa_kernel(
         wkv_blocks = wkv_down.rearrange("(u p e) c -> u e p c", u=2, e=2)
         wq_runs = wq.rearrange("(n a p) c -> n p a c", a=HEADS_PER_RUN, p=P)
 
-        x_raw = []
-        for i in range(TOKEN_BLOCKS):
-            x_raw.append(keep.tile([P, CHANNELS], BF16, name="x_raw%d" % i))
-            nc.sync.dma_start(out=x_raw[i][:], in_=x_blocks[i])
-        wkv_raw = []
-        for t in range(LATENT_BLOCKS):
-            wkv_raw.append(keep.tile([P, CHANNELS], BF16, name="wkv_raw%d" % t))
-            nc.sync.dma_start(out=wkv_raw[t][:], in_=wkv_blocks[t // 2, t % 2])
-        wq_raw = []
-        for run in range(RUNS):
-            wq_raw.append(keep.tile([P, HEADS_PER_RUN, CHANNELS], BF16, name="wq_raw%d" % run))
-            nc.sync.dma_start(out=wq_raw[run][:], in_=wq_runs[run])
+        x_raw = [keep.tile([P, CHANNELS], BF16, name="x_raw%d" % i) for i in range(TOKEN_BLOCKS)]
+        wkv_raw = [keep.tile([P, CHANNELS], BF16, name="wkv_raw%d" % t) for t in range(LATENT_BLOCKS)]
+        wq_raw = [keep.tile([P, HEADS_PER_RUN, CHANNELS], BF16, name="wq_raw%d" % run) for run in range(RUNS)]
+
+        def load(what, n):
+            if what == "x":
+                nc.sync.dma_start(out=x_raw[n][:], in_=x_blocks[n])
+            elif what == "k":
+                nc.sync.dma_start(out=wkv_raw[n][:], in_=wkv_blocks[n // 2, n % 2])
+            else:
+                nc.sync.dma_start(out=wq_raw[n][:], in_=wq_runs[n])
+
+        load("x", 0)
+        load("x", 1)
+        load("x", 2)
+        load("x", 3)
+        load("k", 0)
+        load("k", 1)
+        load("k", 2)
+        load("k", 3)
+        load("w", 0)
+        load("w", 1)
+        load("w", 2)
+        load("w", 3)
+        load("w", 4)
+        load("w", 5)
+        load("w", 6)
+        load("w", 7)
         rotary = keep.tile([P, TOKEN_BLOCKS, 2, 2, PAIRS], BF16)
         nc.scalar.dma_start(out=rotary[:, :, 0, 0, :], in_=cos_view)
         nc.scalar.dma_start(out=rotary[:, :, 1, 0, :], in_=sin_view)
@@ -102,7 +118,11 @@ def tile_attention_pa_kernel(
         def quantise(grouped, codes, scales):
             nc.vector.quantize_mx(out=codes.bitcast(FP8X4), scales=scales, in_=grouped)
 
-        def flip_block(raw, codes, scales):
+        blocks_grouped = {}
+        heads_grouped = {}
+        q_banks = {}
+
+        def flip_block(raw, key):
             words = raw.bitcast(F32)
             grouped = grouped_pool.tile([P, PASSES, P * 4], BF16, name="grouped", align_bytes=64)
             for b in range(PASSES // 2):
@@ -113,6 +133,10 @@ def tile_attention_pa_kernel(
                         "p (s r u) -> p s r u", s=2, u=2
                     ),
                 )
+            blocks_grouped[key] = grouped
+
+        def quantise_block(key, codes, scales):
+            grouped = blocks_grouped[key]
             for b in range(PASSES // 2):
                 passes = slice(2 * b, 2 * b + 2)
                 quantise(
@@ -121,27 +145,28 @@ def tile_attention_pa_kernel(
                     scales[:, passes].rearrange("p s r -> p (s r)"),
                 )
 
-        def flip_heads(run):
-            group, half = divmod(run, GROUP_HEADS // HEADS_PER_RUN)
-            if half == 0:
-                wq_codes[group] = wq_code_pool.tile(
-                    [P, PASSES, GROUP_COLS], U32, name="wq_codes", align_bytes=64
-                )
-                wq_scales[group] = wq_code_pool.tile(
-                    [P, PASSES, GROUP_COLS], U8, name="wq_scales", align_bytes=64
-                )
-            run_cols = HEADS_PER_RUN * HEAD_DIM
-            cols = slice(half * run_cols, (half + 1) * run_cols)
+        def flip_heads(run, passes=range(PASSES)):
             words = [wq_raw[run][:, a, :].bitcast(F32) for a in range(HEADS_PER_RUN)]
-            grouped = grouped_pool.tile([P, PASSES, run_cols * 4], BF16, name="grouped_heads", align_bytes=64)
-            for g in range(PASSES):
+            run_cols = HEADS_PER_RUN * HEAD_DIM
+            if run not in heads_grouped:
+                heads_grouped[run] = grouped_pool.tile([P, PASSES, run_cols * 4], BF16, name="grouped_heads", align_bytes=64)
+            grouped = heads_grouped[run]
+            for g in passes:
                 flip_bank(
                     [w[:, g * 2 * P : (g + 1) * 2 * P] for w in words],
                     grouped[:, g].bitcast(F32).rearrange("p (s r u) -> p s r u", s=2, u=2),
                 )
-            for g in range(PASSES):
+
+        def quantise_heads(run, passes=range(PASSES)):
+            grouped = heads_grouped[run]
+            group, half = divmod(run, GROUP_HEADS // HEADS_PER_RUN)
+            if group not in wq_codes:
+                wq_codes[group] = wq_code_pool.tile([P, PASSES, GROUP_COLS], U32, name="wq_codes", align_bytes=64)
+                wq_scales[group] = wq_code_pool.tile([P, PASSES, GROUP_COLS], U8, name="wq_scales", align_bytes=64)
+            run_cols = HEADS_PER_RUN * HEAD_DIM
+            cols = slice(half * run_cols, (half + 1) * run_cols)
+            for g in passes:
                 quantise(grouped[:, g], wq_codes[group][:, g, cols], wq_scales[group][:, g, cols])
-                finish_deferred()
 
         def rotate(sums, table, rotated):
             count = sums.shape[1]
@@ -166,9 +191,9 @@ def tile_attention_pa_kernel(
 
         deferred = []
 
-        def q_passes(run):
+        def q_passes(run, members=(0, 1)):
             group, half = divmod(run, TOKEN_BLOCKS // BLOCKS_PER_RUN)
-            for i in range(half * BLOCKS_PER_RUN, (half + 1) * BLOCKS_PER_RUN):
+            for i in [half * BLOCKS_PER_RUN + s for s in members]:
                 q_sums = sum_psum.tile([P, GROUP_COLS], F32, name="q_sums", tag="sums")
                 for g in range(PASSES):
                     nc.tensor.matmul_mx(
@@ -180,74 +205,81 @@ def tile_attention_pa_kernel(
                         start=(g == 0),
                         stop=(g == PASSES - 1),
                     )
-                q_rotated = rotated_pool.tile([P, GROUP_HEADS, HEAD_DIM], F32, name="q_rotated")
-                add = rotate(
-                    q_sums[:].rearrange("p (h d) -> p h d", h=GROUP_HEADS), rotary[:, i].unsqueeze(3), q_rotated[:]
+                q_banks[run, i % BLOCKS_PER_RUN] = (group, i, q_sums)
+
+        q_adds = {}
+
+        def q_product(run, s):
+            group, i, q_sums = q_banks[run, s]
+            q_rotated = rotated_pool.tile([P, GROUP_HEADS, HEAD_DIM], F32, name="q_rotated")
+            q_adds[run, s] = (
+                rotate(q_sums[:].rearrange("p (h d) -> p h d", h=GROUP_HEADS), rotary[:, i].unsqueeze(3), q_rotated[:]),
+                q_rotated,
+            )
+
+        def q_add(run, s, engine):
+            group, i, q_sums = q_banks[run, s]
+            add, q_rotated = q_adds[run, s]
+            add(engine)
+            nc.sync.dma_start(
+                out=q_blocks[i][:, group * GROUP_HEADS : (group + 1) * GROUP_HEADS, :],
+                in_=q_rotated[:],
+            )
+
+        signal = keep.tile([P, 4], U32)
+
+        def gpsimd_after_quantise(run):
+            group, half = divmod(run, 2)
+            c = half * 256
+            nc.gpsimd.tensor_copy(out=signal[:], in_=wq_codes[group][:, PASSES - 1, c : c + 4])
+
+        latent_grouped = keep.tile([P, TOKEN_BLOCKS, P * 4], BF16, align_bytes=64)
+
+        latent_banks = {}
+
+        def latent_block(i, t):
+            if i not in latent_banks:
+                latent_banks[i] = sum_psum.tile([P, LATENT_BLOCKS, P], F32, name="latent_sums", tag="sums")
+            for g in range(PASSES):
+                nc.tensor.matmul_mx(
+                    out=latent_banks[i][:, t, :],
+                    lhsT=wkv_codes[:, t, g, :].bitcast(FP8X4),
+                    lhsT_scale=wkv_scales[:, t, g, :],
+                    rhs=x_codes[:, i, g, :].bitcast(FP8X4),
+                    rhs_scale=x_scales[:, i, g, :],
+                    start=(g == 0),
+                    stop=(g == PASSES - 1),
                 )
 
-                def finish(engine, add=add, i=i, q_rotated=q_rotated):
-                    add(engine)
-                    nc.sync.dma_start(
-                        out=q_blocks[i][:, group * GROUP_HEADS : (group + 1) * GROUP_HEADS, :],
-                        in_=q_rotated[:],
-                    )
+        def latent_copy(i):
+            nc.scalar.copy(
+                out=latent_grouped[:, i].rearrange("p (r t) -> p r t", t=LATENT_BLOCKS),
+                in_=latent_banks[i][:].rearrange("p t r -> p r t"),
+            )
 
-                if i % BLOCKS_PER_RUN == 0:
-                    finish(nc.gpsimd)
-                else:
-                    deferred.append(finish)
+        def latent(i):
+            for t in range(LATENT_BLOCKS):
+                latent_block(i, t)
+            latent_copy(i)
 
-        def finish_deferred():
-            while deferred:
-                deferred.pop()(nc.vector)
+        warm = keep.tile([P, 512], BF16)
 
-        def latent_passes(t):
-            for i in range(TOKEN_BLOCKS):
-                for g in range(PASSES):
-                    nc.tensor.matmul_mx(
-                        out=latent_sums[i][:, t, :],
-                        lhsT=wkv_codes[:, t, g, :].bitcast(FP8X4),
-                        lhsT_scale=wkv_scales[:, t, g, :],
-                        rhs=x_codes[:, i, g, :].bitcast(FP8X4),
-                        rhs_scale=x_scales[:, i, g, :],
-                        start=(g == 0),
-                        stop=(g == PASSES - 1),
-                    )
+        def warm_fill():
+            nc.vector.memset(warm[:], 0.0)
 
-        for i in range(TOKEN_BLOCKS):
-            flip_block(x_raw[i][:], x_codes[:, i], x_scales[:, i])
-        nc.vector.tensor_scalar_mul(out=rotary[:, :, 0, 1, :], in0=rotary[:, :, 1, 0, :], scalar1=-1.0)
+        def dummy(n):
+            idle = sum_psum.tile([P, 512], F32, name="idle", tag="sums")
+            for repeat in range(n):
+                nc.tensor.matmul(idle[:], lhsT=warm[:, 0:P], rhs=warm[:], start=True, stop=True)
 
-        latent_sums = [
-            sum_psum.tile([P, LATENT_BLOCKS, P], F32, name="latent_sums%d" % i, tag="sums")
-            for i in range(TOKEN_BLOCKS)
-        ]
-        flip_block(wkv_raw[0][:], wkv_codes[:, 0], wkv_scales[:, 0])
-        for t in range(1, LATENT_BLOCKS):
-            flip_block(wkv_raw[t][:], wkv_codes[:, t], wkv_scales[:, t])
-            latent_passes(t - 1)
-
-        up_grouped = keep.tile([P, 2 * HEAD_DIM * 4], BF16, align_bytes=64)
-        flip_bank(
-            [up_raw[s][:].bitcast(F32) for s in range(2)],
-            up_grouped[:].bitcast(F32).rearrange("p (s r u) -> p s r u", s=2, u=2),
-        )
-        quantise(up_grouped[:], up_codes[:], up_scales[:])
-        flip_heads(0)
-        latent_passes(LATENT_BLOCKS - 1)
-
-        latent_grouped = keep.tile([P, TOKENS * 4], BF16, align_bytes=64)
-        latent_view = latent_grouped[:].rearrange("p (i r t) -> p i r t", i=TOKEN_BLOCKS, t=LATENT_BLOCKS)
-        for i in range(TOKEN_BLOCKS):
-            nc.scalar.copy(out=latent_view[:, i], in_=latent_sums[i][:].rearrange("p t r -> p r t"))
-        quantise(latent_grouped[:], latent_codes[:], latent_scales[:])
-
-        flip_heads(1)
-        flip_heads(2)
+        def latent_quantise(i):
+            rows = slice(i * P, (i + 1) * P)
+            quantise(latent_grouped[:, i], latent_codes[:, rows], latent_scales[:, rows])
 
         k_rotated = keep.tile([P, TOKEN_BLOCKS, HEAD_DIM], F32)
         v_copied = keep.tile([P, TOKEN_BLOCKS, HEAD_DIM], F32)
-        for b in range(TOKEN_BLOCKS // 2):
+
+        def kv(b):
             kv_sums = sum_psum.tile([P, 2, 2, HEAD_DIM], F32, name="kv_sums", tag="sums")
             for w in range(2):
                 cols = slice(w * HEAD_DIM, (w + 1) * HEAD_DIM)
@@ -263,18 +295,137 @@ def tile_attention_pa_kernel(
                         stop=True,
                     )
             blocks = slice(2 * b, 2 * b + 2)
-            rotate(
-                kv_sums[:, 0], rotary[:, blocks].rearrange("p n o e j -> p o e n j"), k_rotated[:, blocks, :]
-            )(nc.gpsimd)
-            nc.scalar.copy(out=v_copied[:, 2 * b : 2 * b + 2, :], in_=kv_sums[:, 1])
-        nc.sync.dma_start(out=k_view, in_=k_rotated[:])
-        nc.sync.dma_start(out=v_view, in_=v_copied[:])
+            nc.scalar.copy(out=v_copied[:, blocks, :], in_=kv_sums[:, 1])
+            nc.sync.dma_start(out=v_view[:, blocks, :], in_=v_copied[:, blocks, :])
+            k_banks[b] = kv_sums
 
+        k_banks = {}
+        k_adds = {}
+
+        def k_product(b):
+            blocks = slice(2 * b, 2 * b + 2)
+            k_adds[b] = rotate(
+                k_banks[b][:, 0], rotary[:, blocks].rearrange("p n o e j -> p o e n j"), k_rotated[:, blocks, :]
+            )
+
+        def k_add(b, engine):
+            blocks = slice(2 * b, 2 * b + 2)
+            k_adds[b](engine)
+            nc.sync.dma_start(out=k_view[:, blocks, :], in_=k_rotated[:, blocks, :])
+
+        def up():
+            up_grouped = keep.tile([P, 2 * HEAD_DIM * 4], BF16, align_bytes=64)
+            flip_bank(
+                [up_raw[s][:].bitcast(F32) for s in range(2)],
+                up_grouped[:].bitcast(F32).rearrange("p (s r u) -> p s r u", s=2, u=2),
+            )
+            quantise(up_grouped[:], up_codes[:], up_scales[:])
+
+        def x_flip(i):
+            flip_block(x_raw[i][:], ("x", i))
+
+        def x_quantise(i):
+            quantise_block(("x", i), x_codes[:, i], x_scales[:, i])
+
+        def k_flip(t):
+            flip_block(wkv_raw[t][:], ("k", t))
+
+        def k_quantise(t):
+            quantise_block(("k", t), wkv_codes[:, t], wkv_scales[:, t])
+
+        def negate_sin():
+            nc.vector.tensor_scalar_mul(out=rotary[:, :, 0, 1, :], in0=rotary[:, :, 1, 0, :], scalar1=-1.0)
+
+        x_flip(0)
+        x_quantise(0)
+        x_flip(1)
+        x_quantise(1)
+        x_flip(2)
+        x_quantise(2)
+        x_flip(3)
+        x_quantise(3)
+        negate_sin()
+        k_flip(0)
+        k_quantise(0)
+        k_flip(1)
+        k_quantise(1)
+        k_flip(2)
+        k_quantise(2)
+        k_flip(3)
+        k_quantise(3)
+        up()
+        flip_heads(0)
+        quantise_heads(0)
+        latent(0)
+        latent(1)
+        flip_heads(1)
+        quantise_heads(1)
+        latent(2)
+        latent_quantise(0)
+        latent_quantise(1)
+        latent(3)
+        kv(0)
+        flip_heads(2)
+        k_product(0)
+        k_add(0, nc.gpsimd)
+        quantise_heads(2)
+        latent_quantise(2)
+        latent_quantise(3)
         q_passes(0)
-        for run in range(3, RUNS):
-            flip_heads(run)
-            q_passes(run - 2)
-        q_passes(RUNS - 2)
-        finish_deferred()
-        q_passes(RUNS - 1)
-        finish_deferred()
+        q_product(0, 0)
+        q_add(0, 0, nc.gpsimd)
+        q_product(0, 1)
+        kv(1)
+        k_product(1)
+        k_add(1, nc.gpsimd)
+        flip_heads(3)
+        quantise_heads(3)
+        gpsimd_after_quantise(3)
+        q_add(0, 1, nc.gpsimd)
+        q_passes(1)
+        q_product(1, 0)
+        q_add(1, 0, nc.gpsimd)
+        q_product(1, 1)
+        flip_heads(4)
+        quantise_heads(4)
+        gpsimd_after_quantise(4)
+        q_add(1, 1, nc.gpsimd)
+        q_passes(2)
+        q_product(2, 0)
+        q_add(2, 0, nc.gpsimd)
+        q_product(2, 1)
+        flip_heads(5)
+        quantise_heads(5)
+        gpsimd_after_quantise(5)
+        q_add(2, 1, nc.gpsimd)
+        q_passes(3)
+        q_product(3, 0)
+        q_add(3, 0, nc.gpsimd)
+        q_product(3, 1)
+        flip_heads(6)
+        quantise_heads(6)
+        gpsimd_after_quantise(6)
+        q_add(3, 1, nc.gpsimd)
+        q_passes(4)
+        q_product(4, 0)
+        q_add(4, 0, nc.gpsimd)
+        q_product(4, 1)
+        flip_heads(7)
+        quantise_heads(7)
+        gpsimd_after_quantise(7)
+        q_add(4, 1, nc.gpsimd)
+        q_passes(5)
+        q_product(5, 0)
+        q_add(5, 0, nc.gpsimd)
+        q_product(5, 1)
+        q_passes(6)
+        q_add(5, 1, nc.gpsimd)
+        q_product(6, 0)
+        q_add(6, 0, nc.gpsimd)
+        q_product(6, 1)
+        q_add(6, 1, nc.vector)
+        q_passes(7)
+        q_product(7, 0)
+        q_add(7, 0, nc.gpsimd)
+        q_product(7, 1)
+        q_add(7, 1, nc.vector)

@@ -174,8 +174,8 @@ def tile_attention_pa_kernel(
             product = product_pool.tile(shape, F32, name="product", tag="product%d" % count)
             nc.vector.tensor_tensor(
                 out=product[:],
-                in0=sums.rearrange("p n (j e) -> p e n j", e=2).unsqueeze(1).to_broadcast(shape),
-                in1=table.to_broadcast(shape),
+                in0=table.to_broadcast(shape),
+                in1=sums.rearrange("p n (j e) -> p e n j", e=2).unsqueeze(1).to_broadcast(shape),
                 op=MULT,
             )
 
@@ -261,16 +261,6 @@ def tile_attention_pa_kernel(
             for t in range(LATENT_BLOCKS):
                 latent_block(i, t)
             latent_copy(i)
-
-        warm = keep.tile([P, 512], BF16)
-
-        def warm_fill():
-            nc.vector.memset(warm[:], 0.0)
-
-        def dummy(n):
-            idle = sum_psum.tile([P, 512], F32, name="idle", tag="sums")
-            for repeat in range(n):
-                nc.tensor.matmul(idle[:], lhsT=warm[:, 0:P], rhs=warm[:], start=True, stop=True)
 
         def latent_quantise(i):
             rows = slice(i * P, (i + 1) * P)

@@ -85,10 +85,10 @@ def tile_attention_pa_kernel(
         load("w", 5)
         load("w", 6)
         load("w", 7)
-        rotary = keep.tile([P, TOKEN_BLOCKS, 2, 2, PAIRS], BF16)
-        nc.scalar.dma_start(out=rotary[:, :, 0, 0, :], in_=cos_view)
-        nc.scalar.dma_start(out=rotary[:, :, 1, 0, :], in_=sin_view)
-        nc.scalar.dma_start(out=rotary[:, :, 1, 1, :], in_=cos_view)
+        cos_raw = keep.tile([P, TOKEN_BLOCKS, PAIRS], BF16)
+        sin_raw = keep.tile([P, TOKEN_BLOCKS, PAIRS], BF16)
+        nc.scalar.dma_start(out=cos_raw[:], in_=cos_view)
+        nc.scalar.dma_start(out=sin_raw[:], in_=sin_view)
         up_raw = []
         for s, weight in enumerate((wk_up, wv_up)):
             up_raw.append(keep.tile([P, LATENT], BF16, name="up_raw%d" % s))
@@ -96,6 +96,12 @@ def tile_attention_pa_kernel(
 
         identity = keep.tile([P, P], F32)
         make_identity(nc, identity[:])
+
+        rotary = keep.tile([P, TOKEN_BLOCKS, 2, PAIRS, 2], BF16)
+        for e, o, source, sign in ((0, 0, cos_raw, 1.0), (0, 1, sin_raw, 1.0), (1, 0, sin_raw, -1.0), (1, 1, cos_raw, 1.0)):
+            nc.gpsimd.tensor_scalar(
+                out=rotary[:, :, e, :, o], in0=source[:], scalar1=sign, scalar2=0.0, op0=MULT, op1=ADD
+            )
 
         x_codes = keep.tile([P, TOKEN_BLOCKS, PASSES, P], U32, align_bytes=64)
         x_scales = keep.tile([P, TOKEN_BLOCKS, PASSES, P], U8, align_bytes=64)
@@ -170,26 +176,24 @@ def tile_attention_pa_kernel(
 
         def rotate(sums, table, rotated):
             count = sums.shape[1]
-            shape = [P, 2, 2, count, PAIRS]
+            shape = [P, 2, count, PAIRS, 2]
             product = product_pool.tile(shape, F32, name="product", tag="product%d" % count)
             nc.vector.tensor_tensor(
                 out=product[:],
                 in0=table.to_broadcast(shape),
-                in1=sums.rearrange("p n (j e) -> p e n j", e=2).unsqueeze(1).to_broadcast(shape),
+                in1=sums.rearrange("p n (j e) -> p e n j", e=2).unsqueeze(4).to_broadcast(shape),
                 op=MULT,
             )
 
             def add(engine):
                 engine.tensor_tensor(
-                    out=rotated.rearrange("p n (j o) -> p n j o", o=2),
-                    in0=product[:, :, 0].rearrange("p o n j -> p n j o"),
-                    in1=product[:, :, 1].rearrange("p o n j -> p n j o"),
+                    out=rotated,
+                    in0=product[:, 0].rearrange("p n j o -> p n (j o)"),
+                    in1=product[:, 1].rearrange("p n j o -> p n (j o)"),
                     op=ADD,
                 )
 
             return add
-
-        deferred = []
 
         def q_passes(run, members=(0, 1)):
             group, half = divmod(run, TOKEN_BLOCKS // BLOCKS_PER_RUN)
@@ -213,7 +217,7 @@ def tile_attention_pa_kernel(
             group, i, q_sums = q_banks[run, s]
             q_rotated = rotated_pool.tile([P, GROUP_HEADS, HEAD_DIM], F32, name="q_rotated")
             q_adds[run, s] = (
-                rotate(q_sums[:].rearrange("p (h d) -> p h d", h=GROUP_HEADS), rotary[:, i].unsqueeze(3), q_rotated[:]),
+                rotate(q_sums[:].rearrange("p (h d) -> p h d", h=GROUP_HEADS), rotary[:, i].unsqueeze(2), q_rotated[:]),
                 q_rotated,
             )
 
@@ -295,7 +299,7 @@ def tile_attention_pa_kernel(
         def k_product(b):
             blocks = slice(2 * b, 2 * b + 2)
             k_adds[b] = rotate(
-                k_banks[b][:, 0], rotary[:, blocks].rearrange("p n o e j -> p o e n j"), k_rotated[:, blocks, :]
+                k_banks[b][:, 0], rotary[:, blocks].rearrange("p n e j o -> p e n j o"), k_rotated[:, blocks, :]
             )
 
         def k_add(b, engine):
@@ -323,9 +327,6 @@ def tile_attention_pa_kernel(
         def k_quantise(t):
             quantise_block(("k", t), wkv_codes[:, t], wkv_scales[:, t])
 
-        def negate_sin():
-            nc.vector.tensor_scalar_mul(out=rotary[:, :, 0, 1, :], in0=rotary[:, :, 1, 0, :], scalar1=-1.0)
-
         x_flip(0)
         x_quantise(0)
         x_flip(1)
@@ -334,7 +335,6 @@ def tile_attention_pa_kernel(
         x_quantise(2)
         x_flip(3)
         x_quantise(3)
-        negate_sin()
         k_flip(0)
         k_quantise(0)
         k_flip(1)

@@ -22,11 +22,8 @@ K_PASS = 512
 PASSES = CHANNELS // K_PASS
 TOKEN_BLOCKS = TOKENS // P
 LATENT_BLOCKS = LATENT // P
-GROUP_HEADS = 4
-GROUPS = HEADS // GROUP_HEADS
-GROUP_COLS = GROUP_HEADS * HEAD_DIM
 HEADS_PER_RUN = 2
-BLOCKS_PER_RUN = 2
+RUN_COLS = HEADS_PER_RUN * HEAD_DIM
 RUNS = HEADS // HEADS_PER_RUN
 
 FLOPS = 2 * TOKENS * CHANNELS * (HEADS * HEAD_DIM + LATENT) + 2 * TOKENS * LATENT * 2 * HEAD_DIM
@@ -39,7 +36,7 @@ def tile_attention_pa_kernel(
     with ExitStack() as ctx:
         keep = ctx.enter_context(tc.tile_pool(name="keep", bufs=1))
         grouped_pool = ctx.enter_context(tc.tile_pool(name="grouped", bufs=4))
-        wq_code_pool = ctx.enter_context(tc.tile_pool(name="wq_code", bufs=2))
+        wq_code_pool = ctx.enter_context(tc.tile_pool(name="wq_code", bufs=4))
         product_pool = ctx.enter_context(tc.tile_pool(name="product", bufs=3))
         rotated_pool = ctx.enter_context(tc.tile_pool(name="rotated", bufs=4))
         flip_psum = ctx.enter_context(tc.psum_pool(name="flip", bufs=4))
@@ -49,9 +46,7 @@ def tile_attention_pa_kernel(
         x_blocks = x.flatten_outer_dims().rearrange("(p i) c -> i p c", i=TOKEN_BLOCKS)
         cos_view = freqs_cos.rearrange("(p i) j -> p i j", i=TOKEN_BLOCKS)
         sin_view = freqs_sin.rearrange("(p i) j -> p i j", i=TOKEN_BLOCKS)
-        q_blocks = out_0.flatten_outer_dims().rearrange(
-            "(p i h) d -> i p h d", i=TOKEN_BLOCKS, h=HEADS
-        )
+        q_view = out_0.flatten_outer_dims().rearrange("(p i h) d -> p i h d", i=TOKEN_BLOCKS, h=HEADS)
         k_view = out_1.flatten_outer_dims().rearrange("(p i) d -> p i d", i=TOKEN_BLOCKS)
         v_view = out_2.flatten_outer_dims().rearrange("(p i) d -> p i d", i=TOKEN_BLOCKS)
         wkv_blocks = wkv_down.rearrange("(u p e) c -> u e p c", u=2, e=2)
@@ -67,18 +62,19 @@ def tile_attention_pa_kernel(
             elif what == "k":
                 nc.sync.dma_start(out=wkv_raw[n][:], in_=wkv_blocks[n // 2, n % 2])
             else:
-                nc.sync.dma_start(out=wq_raw[n][:], in_=wq_runs[n])
+                for channels in (slice(0, CHANNELS // 2), slice(CHANNELS // 2, CHANNELS)):
+                    nc.sync.dma_start(out=wq_raw[n][:, :, channels], in_=wq_runs[n][:, :, channels])
 
         load("x", 0)
         load("x", 1)
+        load("w", 0)
         load("x", 2)
         load("x", 3)
         load("k", 0)
         load("k", 1)
+        load("w", 1)
         load("k", 2)
         load("k", 3)
-        load("w", 0)
-        load("w", 1)
         load("w", 2)
         load("w", 3)
         load("w", 4)
@@ -97,11 +93,20 @@ def tile_attention_pa_kernel(
         identity = keep.tile([P, P], F32)
         make_identity(nc, identity[:])
 
-        rotary = keep.tile([P, TOKEN_BLOCKS, 2, PAIRS, 2], BF16)
+        rotary = keep.tile([P, 2, 2, 2, HEADS_PER_RUN, PAIRS, 2], BF16)
         for e, o, source, sign in ((0, 0, cos_raw, 1.0), (0, 1, sin_raw, 1.0), (1, 0, sin_raw, -1.0), (1, 1, cos_raw, 1.0)):
             nc.gpsimd.tensor_scalar(
-                out=rotary[:, :, e, :, o], in0=source[:], scalar1=sign, scalar2=0.0, op0=MULT, op1=ADD
+                out=rotary[:, :, e, :, 0, :, o],
+                in0=source[:].rearrange("p (b i) j -> p b i j", i=2),
+                scalar1=sign,
+                scalar2=0.0,
+                op0=MULT,
+                op1=ADD,
             )
+        rotary_heads = rotary[:].rearrange("p b e i h j o -> p (b e i) h (j o)")
+        nc.gpsimd.tensor_scalar(
+            out=rotary_heads[:, :, 1], in0=rotary_heads[:, :, 0], scalar1=1.0, scalar2=0.0, op0=MULT, op1=ADD
+        )
 
         x_codes = keep.tile([P, TOKEN_BLOCKS, PASSES, P], U32, align_bytes=64)
         x_scales = keep.tile([P, TOKEN_BLOCKS, PASSES, P], U8, align_bytes=64)
@@ -153,9 +158,8 @@ def tile_attention_pa_kernel(
 
         def flip_heads(run, passes=range(PASSES)):
             words = [wq_raw[run][:, a, :].bitcast(F32) for a in range(HEADS_PER_RUN)]
-            run_cols = HEADS_PER_RUN * HEAD_DIM
             if run not in heads_grouped:
-                heads_grouped[run] = grouped_pool.tile([P, PASSES, run_cols * 4], BF16, name="grouped_heads", align_bytes=64)
+                heads_grouped[run] = grouped_pool.tile([P, PASSES, RUN_COLS * 4], BF16, name="grouped_heads", align_bytes=64)
             grouped = heads_grouped[run]
             for g in passes:
                 flip_bank(
@@ -165,77 +169,70 @@ def tile_attention_pa_kernel(
 
         def quantise_heads(run, passes=range(PASSES)):
             grouped = heads_grouped[run]
-            group, half = divmod(run, GROUP_HEADS // HEADS_PER_RUN)
-            if group not in wq_codes:
-                wq_codes[group] = wq_code_pool.tile([P, PASSES, GROUP_COLS], U32, name="wq_codes", align_bytes=64)
-                wq_scales[group] = wq_code_pool.tile([P, PASSES, GROUP_COLS], U8, name="wq_scales", align_bytes=64)
-            run_cols = HEADS_PER_RUN * HEAD_DIM
-            cols = slice(half * run_cols, (half + 1) * run_cols)
+            if run not in wq_codes:
+                wq_codes[run] = wq_code_pool.tile([P, PASSES, RUN_COLS], U32, name="wq_codes", align_bytes=64)
+                wq_scales[run] = wq_code_pool.tile([P, PASSES, RUN_COLS], U8, name="wq_scales", align_bytes=64)
             for g in passes:
-                quantise(grouped[:, g], wq_codes[group][:, g, cols], wq_scales[group][:, g, cols])
+                quantise(grouped[:, g], wq_codes[run][:, g, :], wq_scales[run][:, g, :])
 
-        def rotate(sums, table, rotated):
-            count = sums.shape[1]
-            shape = [P, 2, count, PAIRS, 2]
-            product = product_pool.tile(shape, F32, name="product", tag="product%d" % count)
+        def rotate(sums, table, name):
+            product = product_pool.tile(table.shape, F32, name=name)
+            planes = sums.rearrange("p (n e) -> p e n", e=2)
+            if len(table.shape) == 5:
+                planes = planes.rearrange("p e (n j) -> p e n j", n=2)
             nc.vector.tensor_tensor(
                 out=product[:],
-                in0=table.to_broadcast(shape),
-                in1=sums.rearrange("p n (j e) -> p e n j", e=2).unsqueeze(4).to_broadcast(shape),
+                in0=planes.unsqueeze(len(table.shape) - 1).to_broadcast(table.shape),
+                in1=table,
                 op=MULT,
             )
+            return product
 
-            def add(engine):
-                engine.tensor_tensor(
-                    out=rotated,
-                    in0=product[:, 0].rearrange("p n j o -> p n (j o)"),
-                    in1=product[:, 1].rearrange("p n j o -> p n (j o)"),
-                    op=ADD,
-                )
-
-            return add
+        def add_planes(product, rotated, engine):
+            flat = product[:]
+            if len(product.shape) == 5:
+                flat = flat.rearrange("p e n j o -> p e (n j) o")
+            engine.tensor_tensor(
+                out=rotated,
+                in0=flat[:, 0].rearrange("p n o -> p (n o)"),
+                in1=flat[:, 1].rearrange("p n o -> p (n o)"),
+                op=ADD,
+            )
 
         def q_passes(run, members=(0, 1)):
-            group, half = divmod(run, TOKEN_BLOCKS // BLOCKS_PER_RUN)
-            for i in [half * BLOCKS_PER_RUN + s for s in members]:
-                q_sums = sum_psum.tile([P, GROUP_COLS], F32, name="q_sums", tag="sums")
-                for g in range(PASSES):
-                    nc.tensor.matmul_mx(
-                        out=q_sums[:],
-                        lhsT=x_codes[:, i, g, :].bitcast(FP8X4),
-                        lhsT_scale=x_scales[:, i, g, :],
-                        rhs=wq_codes[group][:, g, :].bitcast(FP8X4),
-                        rhs_scale=wq_scales[group][:, g, :],
-                        start=(g == 0),
-                        stop=(g == PASSES - 1),
-                    )
-                q_banks[run, i % BLOCKS_PER_RUN] = (group, i, q_sums)
+            for b in members:
+                q_sums = sum_psum.tile([P, 2, RUN_COLS], F32, name="q_sums", tag="sums")
+                for i in range(2):
+                    for g in range(PASSES):
+                        nc.tensor.matmul_mx(
+                            out=q_sums[:, i, :],
+                            lhsT=x_codes[:, 2 * b + i, g, :].bitcast(FP8X4),
+                            lhsT_scale=x_scales[:, 2 * b + i, g, :],
+                            rhs=wq_codes[run][:, g, :].bitcast(FP8X4),
+                            rhs_scale=wq_scales[run][:, g, :],
+                            start=(g == 0),
+                            stop=(g == PASSES - 1),
+                        )
+                q_banks[run, b] = q_sums
 
-        q_adds = {}
+        q_products = {}
 
-        def q_product(run, s):
-            group, i, q_sums = q_banks[run, s]
-            q_rotated = rotated_pool.tile([P, GROUP_HEADS, HEAD_DIM], F32, name="q_rotated")
-            q_adds[run, s] = (
-                rotate(q_sums[:].rearrange("p (h d) -> p h d", h=GROUP_HEADS), rotary[:, i].unsqueeze(2), q_rotated[:]),
-                q_rotated,
+        def q_product(run, b):
+            q_products[run, b] = rotate(
+                q_banks[run, b][:].rearrange("p i c -> p (i c)"),
+                rotary[:, b].rearrange("p e i h j o -> p e (i h j) o"),
+                "product",
             )
 
-        def q_add(run, s, engine):
-            group, i, q_sums = q_banks[run, s]
-            add, q_rotated = q_adds[run, s]
-            add(engine)
+        def q_add(run, b, engine):
+            q_rotated = rotated_pool.tile([P, 2 * RUN_COLS], F32, name="q_rotated")
+            add_planes(q_products[run, b], q_rotated[:], engine)
             nc.sync.dma_start(
-                out=q_blocks[i][:, group * GROUP_HEADS : (group + 1) * GROUP_HEADS, :],
-                in_=q_rotated[:],
+                out=q_view[:, 2 * b : 2 * b + 2, run * HEADS_PER_RUN : (run + 1) * HEADS_PER_RUN, :].rearrange(
+                    "p i h d -> p i (h d)"
+                ),
+                in_=q_rotated[:].rearrange("p (i c) -> p i c", i=2),
             )
-
-        signal = keep.tile([P, 4], U32)
-
-        def gpsimd_after_quantise(run):
-            group, half = divmod(run, 2)
-            c = half * 256
-            nc.gpsimd.tensor_copy(out=signal[:], in_=wq_codes[group][:, PASSES - 1, c : c + 4])
 
         latent_grouped = keep.tile([P, TOKEN_BLOCKS, P * 4], BF16, align_bytes=64)
 
@@ -297,14 +294,13 @@ def tile_attention_pa_kernel(
         k_adds = {}
 
         def k_product(b):
-            blocks = slice(2 * b, 2 * b + 2)
             k_adds[b] = rotate(
-                k_banks[b][:, 0], rotary[:, blocks].rearrange("p n e j o -> p e n j o"), k_rotated[:, blocks, :]
+                k_banks[b][:, 0].rearrange("p s d -> p (s d)"), rotary[:, b, :, :, 0], "product_k"
             )
 
         def k_add(b, engine):
             blocks = slice(2 * b, 2 * b + 2)
-            k_adds[b](engine)
+            add_planes(k_adds[b], k_rotated[:, blocks, :].rearrange("p s d -> p (s d)"), engine)
             nc.sync.dma_start(out=k_view[:, blocks, :], in_=k_rotated[:, blocks, :])
 
         def up():
@@ -331,6 +327,8 @@ def tile_attention_pa_kernel(
         x_quantise(0)
         x_flip(1)
         x_quantise(1)
+        flip_heads(0)
+        quantise_heads(0)
         x_flip(2)
         x_quantise(2)
         x_flip(3)
@@ -339,83 +337,76 @@ def tile_attention_pa_kernel(
         k_quantise(0)
         k_flip(1)
         k_quantise(1)
+        q_passes(0)
+        q_product(0, 0)
+        q_product(0, 1)
+        q_add(0, 0, nc.vector)
+        flip_heads(1)
+        quantise_heads(1)
+        q_add(0, 1, nc.vector)
         k_flip(2)
         k_quantise(2)
         k_flip(3)
         k_quantise(3)
         up()
-        flip_heads(0)
-        quantise_heads(0)
-        latent(0)
-        latent(1)
-        flip_heads(1)
-        quantise_heads(1)
-        latent(2)
-        latent_quantise(0)
-        latent_quantise(1)
-        latent(3)
-        kv(0)
-        flip_heads(2)
-        k_product(0)
-        k_add(0, nc.gpsimd)
-        quantise_heads(2)
-        latent_quantise(2)
-        latent_quantise(3)
-        q_passes(0)
-        q_product(0, 0)
-        q_add(0, 0, nc.gpsimd)
-        q_product(0, 1)
-        kv(1)
-        k_product(1)
-        k_add(1, nc.gpsimd)
-        flip_heads(3)
-        quantise_heads(3)
-        gpsimd_after_quantise(3)
-        q_add(0, 1, nc.gpsimd)
         q_passes(1)
         q_product(1, 0)
-        q_add(1, 0, nc.gpsimd)
         q_product(1, 1)
-        flip_heads(4)
-        quantise_heads(4)
-        gpsimd_after_quantise(4)
-        q_add(1, 1, nc.gpsimd)
+        q_add(1, 0, nc.vector)
+        flip_heads(2)
+        quantise_heads(2)
+        q_add(1, 1, nc.vector)
+        latent(0)
+        latent_quantise(0)
+        flip_heads(3)
+        quantise_heads(3)
         q_passes(2)
         q_product(2, 0)
-        q_add(2, 0, nc.gpsimd)
         q_product(2, 1)
-        flip_heads(5)
-        quantise_heads(5)
-        gpsimd_after_quantise(5)
-        q_add(2, 1, nc.gpsimd)
+        q_add(2, 0, nc.vector)
+        flip_heads(4)
+        quantise_heads(4)
+        q_add(2, 1, nc.vector)
+        latent(1)
+        latent_quantise(1)
         q_passes(3)
         q_product(3, 0)
-        q_add(3, 0, nc.gpsimd)
         q_product(3, 1)
-        flip_heads(6)
-        quantise_heads(6)
-        gpsimd_after_quantise(6)
-        q_add(3, 1, nc.gpsimd)
+        kv(0)
+        k_product(0)
+        q_add(3, 0, nc.vector)
+        flip_heads(5)
+        quantise_heads(5)
         q_passes(4)
         q_product(4, 0)
-        q_add(4, 0, nc.gpsimd)
         q_product(4, 1)
-        flip_heads(7)
-        quantise_heads(7)
-        gpsimd_after_quantise(7)
-        q_add(4, 1, nc.gpsimd)
+        q_add(3, 1, nc.vector)
+        latent(2)
+        latent_quantise(2)
+        q_add(4, 0, nc.vector)
+        q_add(4, 1, nc.vector)
+        flip_heads(6)
+        quantise_heads(6)
         q_passes(5)
         q_product(5, 0)
-        q_add(5, 0, nc.gpsimd)
         q_product(5, 1)
+        q_add(5, 0, nc.vector)
+        latent(3)
+        latent_quantise(3)
+        q_add(5, 1, nc.vector)
+        k_add(0, nc.vector)
+        flip_heads(7)
+        quantise_heads(7)
         q_passes(6)
-        q_add(5, 1, nc.gpsimd)
         q_product(6, 0)
-        q_add(6, 0, nc.gpsimd)
         q_product(6, 1)
-        q_add(6, 1, nc.vector)
+        kv(1)
         q_passes(7)
+        q_add(6, 0, nc.vector)
+        q_add(6, 1, nc.vector)
         q_product(7, 0)
-        q_add(7, 0, nc.gpsimd)
         q_product(7, 1)
+        k_product(1)
+        q_add(7, 0, nc.vector)
         q_add(7, 1, nc.vector)
+        k_add(1, nc.vector)

@@ -22,9 +22,11 @@ K_PASS = 512
 PASSES = CHANNELS // K_PASS
 TOKEN_BLOCKS = TOKENS // P
 LATENT_BLOCKS = LATENT // P
-HEADS_PER_RUN = 2
-RUN_COLS = HEADS_PER_RUN * HEAD_DIM
-RUNS = HEADS // HEADS_PER_RUN
+RUN_HEADS = 2
+RUNS = HEADS // RUN_HEADS
+RUN_COLS = RUN_HEADS * HEAD_DIM
+BUSY_COLS = 512
+FIRST, SECOND = (0, 1), (2, 3)
 
 FLOPS = 2 * TOKENS * CHANNELS * (HEADS * HEAD_DIM + LATENT) + 2 * TOKENS * LATENT * 2 * HEAD_DIM
 
@@ -35,11 +37,12 @@ def tile_attention_pa_kernel(
     nc = tc.nc
     with ExitStack() as ctx:
         keep = ctx.enter_context(tc.tile_pool(name="keep", bufs=1))
-        grouped_pool = ctx.enter_context(tc.tile_pool(name="grouped", bufs=4))
-        wq_code_pool = ctx.enter_context(tc.tile_pool(name="wq_code", bufs=4))
-        product_pool = ctx.enter_context(tc.tile_pool(name="product", bufs=3))
-        rotated_pool = ctx.enter_context(tc.tile_pool(name="rotated", bufs=4))
-        flip_psum = ctx.enter_context(tc.psum_pool(name="flip", bufs=4))
+        block_pool = ctx.enter_context(tc.tile_pool(name="block_words", bufs=4))
+        heads_pool = ctx.enter_context(tc.tile_pool(name="heads_words", bufs=3))
+        wq_code_pool = ctx.enter_context(tc.tile_pool(name="wq_codes", bufs=4))
+        product_pool = ctx.enter_context(tc.tile_pool(name="products", bufs=3))
+        rotated_pool = ctx.enter_context(tc.tile_pool(name="rotated", bufs=8))
+        flip_psum = ctx.enter_context(tc.psum_pool(name="flips", bufs=4))
         sum_psum = ctx.enter_context(tc.psum_pool(name="sums", bufs=4))
         ctx.enter_context(tc.manual_schedule())
 
@@ -50,37 +53,34 @@ def tile_attention_pa_kernel(
         k_view = out_1.flatten_outer_dims().rearrange("(p i) d -> p i d", i=TOKEN_BLOCKS)
         v_view = out_2.flatten_outer_dims().rearrange("(p i) d -> p i d", i=TOKEN_BLOCKS)
         wkv_blocks = wkv_down.rearrange("(u p e) c -> u e p c", u=2, e=2)
-        wq_runs = wq.rearrange("(n a p) c -> n p a c", a=HEADS_PER_RUN, p=P)
+        wq_runs = wq.rearrange("(n a p) c -> n p a c", a=RUN_HEADS, p=P)
 
         x_raw = [keep.tile([P, CHANNELS], BF16, name="x_raw%d" % i) for i in range(TOKEN_BLOCKS)]
         wkv_raw = [keep.tile([P, CHANNELS], BF16, name="wkv_raw%d" % t) for t in range(LATENT_BLOCKS)]
-        wq_raw = [keep.tile([P, HEADS_PER_RUN, CHANNELS], BF16, name="wq_raw%d" % run) for run in range(RUNS)]
+        wq_raw = [keep.tile([P, RUN_HEADS, CHANNELS], BF16, name="wq_raw%d" % run) for run in range(RUNS)]
 
-        def load(what, n):
-            if what == "x":
-                nc.sync.dma_start(out=x_raw[n][:], in_=x_blocks[n])
-            elif what == "k":
-                nc.sync.dma_start(out=wkv_raw[n][:], in_=wkv_blocks[n // 2, n % 2])
-            else:
-                for channels in (slice(0, CHANNELS // 2), slice(CHANNELS // 2, CHANNELS)):
-                    nc.sync.dma_start(out=wq_raw[n][:, :, channels], in_=wq_runs[n][:, :, channels])
+        def load_x(i):
+            nc.sync.dma_start(out=x_raw[i][:], in_=x_blocks[i])
 
-        load("x", 0)
-        load("x", 1)
-        load("w", 0)
-        load("x", 2)
-        load("x", 3)
-        load("k", 0)
-        load("k", 1)
-        load("w", 1)
-        load("k", 2)
-        load("k", 3)
-        load("w", 2)
-        load("w", 3)
-        load("w", 4)
-        load("w", 5)
-        load("w", 6)
-        load("w", 7)
+        def load_wkv(t):
+            nc.sync.dma_start(out=wkv_raw[t][:], in_=wkv_blocks[t // 2, t % 2])
+
+        def load_heads(run):
+            for channels in (slice(0, CHANNELS // 2), slice(CHANNELS // 2, CHANNELS)):
+                nc.sync.dma_start(out=wq_raw[run][:, :, channels], in_=wq_runs[run][:, :, channels])
+
+        load_x(0)
+        load_x(1)
+        load_heads(0)
+        load_x(2)
+        load_x(3)
+        load_wkv(0)
+        load_wkv(1)
+        load_heads(1)
+        load_wkv(2)
+        load_wkv(3)
+        for run in range(2, RUNS):
+            load_heads(run)
         cos_raw = keep.tile([P, TOKEN_BLOCKS, PAIRS], BF16)
         sin_raw = keep.tile([P, TOKEN_BLOCKS, PAIRS], BF16)
         nc.scalar.dma_start(out=cos_raw[:], in_=cos_view)
@@ -90,10 +90,14 @@ def tile_attention_pa_kernel(
             up_raw.append(keep.tile([P, LATENT], BF16, name="up_raw%d" % s))
             nc.scalar.dma_start(out=up_raw[s][:], in_=weight)
 
+        busy = keep.tile([P, BUSY_COLS], BF16)
+        nc.gpsimd.iota(
+            busy[:], pattern=[[7, BUSY_COLS]], base=-1792, channel_multiplier=5, allow_small_or_imprecise_dtypes=True
+        )
         identity = keep.tile([P, P], F32)
         make_identity(nc, identity[:])
 
-        rotary = keep.tile([P, 2, 2, 2, HEADS_PER_RUN, PAIRS, 2], BF16)
+        rotary = keep.tile([P, 2, 2, 2, RUN_HEADS, PAIRS, 2], BF16)
         for e, o, source, sign in ((0, 0, cos_raw, 1.0), (0, 1, sin_raw, 1.0), (1, 0, sin_raw, -1.0), (1, 1, cos_raw, 1.0)):
             nc.gpsimd.tensor_scalar(
                 out=rotary[:, :, e, :, 0, :, o],
@@ -114,299 +118,242 @@ def tile_attention_pa_kernel(
         wkv_scales = keep.tile([P, LATENT_BLOCKS, PASSES, P], U8, align_bytes=64)
         up_codes = keep.tile([P, 2 * HEAD_DIM], U32, align_bytes=64)
         up_scales = keep.tile([P, 2 * HEAD_DIM], U8, align_bytes=64)
+        latent_words = keep.tile([P, TOKEN_BLOCKS, P * 4], BF16, align_bytes=64)
         latent_codes = keep.tile([P, TOKENS], U32, align_bytes=64)
         latent_scales = keep.tile([P, TOKENS], U8, align_bytes=64)
         wq_codes = {}
         wq_scales = {}
 
-        def flip_bank(slabs, grouped_words):
+        def flip_bank(slabs, words):
             bank = flip_psum.tile([P, 2, 2, P], F32, name="bank")
             for s in range(2):
                 for u in range(2):
                     nc.tensor.transpose(bank[:, s, u, :], slabs[s][:, u * P : (u + 1) * P], identity[:])
-            nc.scalar.copy(out=grouped_words, in_=bank[:].rearrange("p s u r -> p s r u"))
+            nc.scalar.copy(
+                out=words.bitcast(F32).rearrange("p (s r u) -> p s r u", s=2, u=2),
+                in_=bank[:].rearrange("p s u r -> p s r u"),
+            )
 
-        def quantise(grouped, codes, scales):
-            nc.vector.quantize_mx(out=codes.bitcast(FP8X4), scales=scales, in_=grouped)
+        def quantise(words, codes, scales):
+            nc.vector.quantize_mx(out=codes.bitcast(FP8X4), scales=scales, in_=words)
 
-        blocks_grouped = {}
-        heads_grouped = {}
-        q_banks = {}
-
-        def flip_block(raw, key):
-            words = raw.bitcast(F32)
-            grouped = grouped_pool.tile([P, PASSES, P * 4], BF16, name="grouped", align_bytes=64)
-            for b in range(PASSES // 2):
-                passes = slice(2 * b, 2 * b + 2)
+        def flip_block(raw, codes, scales):
+            channels = raw.bitcast(F32).rearrange("p (g w) -> p g w", g=PASSES)
+            words = block_pool.tile([P, PASSES, P * 4], BF16, name="block_words", align_bytes=64)
+            for g in range(0, PASSES, 2):
                 flip_bank(
-                    [words[:, g * 2 * P : (g + 1) * 2 * P] for g in (2 * b, 2 * b + 1)],
-                    grouped[:, passes].rearrange("p s w -> p (s w)").bitcast(F32).rearrange(
-                        "p (s r u) -> p s r u", s=2, u=2
-                    ),
+                    [channels[:, g], channels[:, g + 1]], words[:, g : g + 2].rearrange("p s w -> p (s w)")
                 )
-            blocks_grouped[key] = grouped
-
-        def quantise_block(key, codes, scales):
-            grouped = blocks_grouped[key]
-            for b in range(PASSES // 2):
-                passes = slice(2 * b, 2 * b + 2)
+            for g in range(0, PASSES, 2):
                 quantise(
-                    grouped[:, passes].rearrange("p s w -> p (s w)"),
-                    codes[:, passes].rearrange("p s r -> p (s r)"),
-                    scales[:, passes].rearrange("p s r -> p (s r)"),
+                    words[:, g : g + 2].rearrange("p s w -> p (s w)"),
+                    codes[:, g : g + 2].rearrange("p s r -> p (s r)"),
+                    scales[:, g : g + 2].rearrange("p s r -> p (s r)"),
                 )
 
-        def flip_heads(run, passes=range(PASSES)):
-            words = [wq_raw[run][:, a, :].bitcast(F32) for a in range(HEADS_PER_RUN)]
-            if run not in heads_grouped:
-                heads_grouped[run] = grouped_pool.tile([P, PASSES, RUN_COLS * 4], BF16, name="grouped_heads", align_bytes=64)
-            grouped = heads_grouped[run]
-            for g in passes:
-                flip_bank(
-                    [w[:, g * 2 * P : (g + 1) * 2 * P] for w in words],
-                    grouped[:, g].bitcast(F32).rearrange("p (s r u) -> p s r u", s=2, u=2),
-                )
+        def flip_x(i):
+            flip_block(x_raw[i][:], x_codes[:, i], x_scales[:, i])
 
-        def quantise_heads(run, passes=range(PASSES)):
-            grouped = heads_grouped[run]
-            if run not in wq_codes:
-                wq_codes[run] = wq_code_pool.tile([P, PASSES, RUN_COLS], U32, name="wq_codes", align_bytes=64)
-                wq_scales[run] = wq_code_pool.tile([P, PASSES, RUN_COLS], U8, name="wq_scales", align_bytes=64)
-            for g in passes:
-                quantise(grouped[:, g], wq_codes[run][:, g, :], wq_scales[run][:, g, :])
+        def flip_wkv(t):
+            flip_block(wkv_raw[t][:], wkv_codes[:, t], wkv_scales[:, t])
 
-        def rotate(sums, table, name):
-            product = product_pool.tile(table.shape, F32, name=name)
-            planes = sums.rearrange("p (n e) -> p e n", e=2)
-            if len(table.shape) == 5:
-                planes = planes.rearrange("p e (n j) -> p e n j", n=2)
+        def flip_heads(run):
+            heads = [
+                wq_raw[run][:, a, :].bitcast(F32).rearrange("p (g w) -> p g w", g=PASSES) for a in range(RUN_HEADS)
+            ]
+            words = heads_pool.tile([P, PASSES, RUN_COLS * 4], BF16, name="heads_words", align_bytes=64)
+            for g in range(PASSES):
+                flip_bank([head[:, g] for head in heads], words[:, g])
+            wq_codes[run] = wq_code_pool.tile([P, PASSES, RUN_COLS], U32, name="run_codes", align_bytes=64)
+            wq_scales[run] = wq_code_pool.tile([P, PASSES, RUN_COLS], U8, name="run_scales", align_bytes=64)
+            for g in range(PASSES):
+                quantise(words[:, g], wq_codes[run][:, g, :], wq_scales[run][:, g, :])
+
+        def flip_up():
+            words = keep.tile([P, 2 * HEAD_DIM * 4], BF16, align_bytes=64)
+            flip_bank([up_raw[s][:].bitcast(F32) for s in range(2)], words[:])
+            quantise(words[:], up_codes[:], up_scales[:])
+
+        def form_products(sums, table, products):
             nc.vector.tensor_tensor(
-                out=product[:],
-                in0=planes.unsqueeze(len(table.shape) - 1).to_broadcast(table.shape),
-                in1=table,
-                op=MULT,
-            )
-            return product
-
-        def add_planes(product, rotated, engine):
-            flat = product[:]
-            if len(product.shape) == 5:
-                flat = flat.rearrange("p e n j o -> p e (n j) o")
-            engine.tensor_tensor(
-                out=rotated,
-                in0=flat[:, 0].rearrange("p n o -> p (n o)"),
-                in1=flat[:, 1].rearrange("p n o -> p (n o)"),
-                op=ADD,
+                out=products, in0=sums.unsqueeze(len(table.shape) - 1).to_broadcast(table.shape), in1=table, op=MULT
             )
 
-        def q_passes(run, members=(0, 1)):
-            for b in members:
-                q_sums = sum_psum.tile([P, 2, RUN_COLS], F32, name="q_sums", tag="sums")
-                for i in range(2):
-                    for g in range(PASSES):
-                        nc.tensor.matmul_mx(
-                            out=q_sums[:, i, :],
-                            lhsT=x_codes[:, 2 * b + i, g, :].bitcast(FP8X4),
-                            lhsT_scale=x_scales[:, 2 * b + i, g, :],
-                            rhs=wq_codes[run][:, g, :].bitcast(FP8X4),
-                            rhs_scale=wq_scales[run][:, g, :],
-                            start=(g == 0),
-                            stop=(g == PASSES - 1),
-                        )
-                q_banks[run, b] = q_sums
+        def add_planes(engine, products, rotated):
+            engine.tensor_tensor(out=rotated, in0=products[:, 0], in1=products[:, 1], op=ADD)
 
+        q_sums = {}
         q_products = {}
 
-        def q_product(run, b):
-            q_products[run, b] = rotate(
-                q_banks[run, b][:].rearrange("p i c -> p (i c)"),
-                rotary[:, b].rearrange("p e i h j o -> p e (i h j) o"),
-                "product",
-            )
+        def q_passes(run, blocks):
+            bank = sum_psum.tile([P, len(blocks), RUN_COLS], F32, name="q_sums", tag="sums")
+            for s, i in enumerate(blocks):
+                for g in range(PASSES):
+                    nc.tensor.matmul_mx(
+                        out=bank[:, s, :],
+                        lhsT=x_codes[:, i, g, :].bitcast(FP8X4),
+                        lhsT_scale=x_scales[:, i, g, :],
+                        rhs=wq_codes[run][:, g, :].bitcast(FP8X4),
+                        rhs_scale=wq_scales[run][:, g, :],
+                        start=(g == 0),
+                        stop=(g == PASSES - 1),
+                    )
+            q_sums[run, blocks] = bank
 
-        def q_add(run, b, engine):
-            q_rotated = rotated_pool.tile([P, 2 * RUN_COLS], F32, name="q_rotated")
-            add_planes(q_products[run, b], q_rotated[:], engine)
+        def q_product(run, blocks):
+            b, i = divmod(blocks[0], 2)
+            products = product_pool.tile([P, 2, len(blocks) * RUN_COLS], F32, name="q_products%d" % len(blocks), bufs=1 + len(blocks))
+            form_products(
+                q_sums[run, blocks][:].rearrange("p s (n e) -> p e (s n)", e=2),
+                rotary[:, b, :, i : i + len(blocks)].rearrange("p e i h j o -> p e (i h j) o"),
+                products[:].rearrange("p e (n o) -> p e n o", o=2),
+            )
+            q_products[run, blocks] = products
+
+        def q_add(engine, run, blocks):
+            rotated = rotated_pool.tile([P, len(blocks) * RUN_COLS], F32, name="q_rotated%d" % len(blocks), bufs=8 if blocks in (FIRST, SECOND) else 2)
+            add_planes(engine, q_products[run, blocks][:], rotated[:])
+            heads = slice(run * RUN_HEADS, (run + 1) * RUN_HEADS)
             nc.sync.dma_start(
-                out=q_view[:, 2 * b : 2 * b + 2, run * HEADS_PER_RUN : (run + 1) * HEADS_PER_RUN, :].rearrange(
-                    "p i h d -> p i (h d)"
-                ),
-                in_=q_rotated[:].rearrange("p (i c) -> p i c", i=2),
+                out=q_view[:, blocks[0] : blocks[-1] + 1, heads, :].rearrange("p i h d -> p i (h d)"),
+                in_=rotated[:].rearrange("p (i c) -> p i c", i=len(blocks)),
             )
 
-        latent_grouped = keep.tile([P, TOKEN_BLOCKS, P * 4], BF16, align_bytes=64)
-
-        latent_banks = {}
-
-        def latent_block(i, t):
-            if i not in latent_banks:
-                latent_banks[i] = sum_psum.tile([P, LATENT_BLOCKS, P], F32, name="latent_sums", tag="sums")
-            for g in range(PASSES):
-                nc.tensor.matmul_mx(
-                    out=latent_banks[i][:, t, :],
-                    lhsT=wkv_codes[:, t, g, :].bitcast(FP8X4),
-                    lhsT_scale=wkv_scales[:, t, g, :],
-                    rhs=x_codes[:, i, g, :].bitcast(FP8X4),
-                    rhs_scale=x_scales[:, i, g, :],
-                    start=(g == 0),
-                    stop=(g == PASSES - 1),
-                )
-
-        def latent_copy(i):
-            nc.scalar.copy(
-                out=latent_grouped[:, i].rearrange("p (r t) -> p r t", t=LATENT_BLOCKS),
-                in_=latent_banks[i][:].rearrange("p t r -> p r t"),
-            )
-
-        def latent(i):
+        def latent_passes(i):
+            bank = sum_psum.tile([P, LATENT_BLOCKS, P], F32, name="latent_sums", tag="sums")
             for t in range(LATENT_BLOCKS):
-                latent_block(i, t)
-            latent_copy(i)
+                for g in range(PASSES):
+                    nc.tensor.matmul_mx(
+                        out=bank[:, t, :],
+                        lhsT=wkv_codes[:, t, g, :].bitcast(FP8X4),
+                        lhsT_scale=wkv_scales[:, t, g, :],
+                        rhs=x_codes[:, i, g, :].bitcast(FP8X4),
+                        rhs_scale=x_scales[:, i, g, :],
+                        start=(g == 0),
+                        stop=(g == PASSES - 1),
+                    )
+            nc.scalar.copy(
+                out=latent_words[:, i].rearrange("p (r t) -> p r t", t=LATENT_BLOCKS),
+                in_=bank[:].rearrange("p t r -> p r t"),
+            )
 
         def latent_quantise(i):
-            rows = slice(i * P, (i + 1) * P)
-            quantise(latent_grouped[:, i], latent_codes[:, rows], latent_scales[:, rows])
+            tokens = slice(i * P, (i + 1) * P)
+            quantise(latent_words[:, i], latent_codes[:, tokens], latent_scales[:, tokens])
 
-        k_rotated = keep.tile([P, TOKEN_BLOCKS, HEAD_DIM], F32)
-        v_copied = keep.tile([P, TOKEN_BLOCKS, HEAD_DIM], F32)
+        k_sums = {}
 
-        def kv(b):
-            kv_sums = sum_psum.tile([P, 2, 2, HEAD_DIM], F32, name="kv_sums", tag="sums")
+        def kv_passes(b):
+            bank = sum_psum.tile([P, 2, 2, HEAD_DIM], F32, name="kv_sums", tag="sums")
             for w in range(2):
-                cols = slice(w * HEAD_DIM, (w + 1) * HEAD_DIM)
+                columns = slice(w * HEAD_DIM, (w + 1) * HEAD_DIM)
                 for s in range(2):
                     tokens = slice((2 * b + s) * P, (2 * b + s + 1) * P)
                     nc.tensor.matmul_mx(
-                        out=kv_sums[:, w, s, :],
+                        out=bank[:, w, s, :],
                         lhsT=latent_codes[:, tokens].bitcast(FP8X4),
                         lhsT_scale=latent_scales[:, tokens],
-                        rhs=up_codes[:, cols].bitcast(FP8X4),
-                        rhs_scale=up_scales[:, cols],
+                        rhs=up_codes[:, columns].bitcast(FP8X4),
+                        rhs_scale=up_scales[:, columns],
                         start=True,
                         stop=True,
                     )
-            blocks = slice(2 * b, 2 * b + 2)
-            nc.scalar.copy(out=v_copied[:, blocks, :], in_=kv_sums[:, 1])
-            nc.sync.dma_start(out=v_view[:, blocks, :], in_=v_copied[:, blocks, :])
-            k_banks[b] = kv_sums
+            v_copied = rotated_pool.tile([P, 2, HEAD_DIM], F32, name="v_copied", bufs=2)
+            nc.scalar.copy(out=v_copied[:], in_=bank[:, 1])
+            nc.sync.dma_start(out=v_view[:, 2 * b : 2 * b + 2, :], in_=v_copied[:])
+            k_sums[b] = bank
 
-        k_banks = {}
-        k_adds = {}
+        k_products = {}
 
         def k_product(b):
-            k_adds[b] = rotate(
-                k_banks[b][:, 0].rearrange("p s d -> p (s d)"), rotary[:, b, :, :, 0], "product_k"
+            k_products[b] = product_pool.tile([P, 2, 2 * HEAD_DIM], F32, name="k_products", bufs=2)
+            form_products(
+                k_sums[b][:, 0].rearrange("p s (j e) -> p e s j", e=2),
+                rotary[:, b, :, :, 0],
+                k_products[b][:].rearrange("p e (s j o) -> p e s j o", s=2, o=2),
             )
 
-        def k_add(b, engine):
-            blocks = slice(2 * b, 2 * b + 2)
-            add_planes(k_adds[b], k_rotated[:, blocks, :].rearrange("p s d -> p (s d)"), engine)
-            nc.sync.dma_start(out=k_view[:, blocks, :], in_=k_rotated[:, blocks, :])
-
-        def up():
-            up_grouped = keep.tile([P, 2 * HEAD_DIM * 4], BF16, align_bytes=64)
-            flip_bank(
-                [up_raw[s][:].bitcast(F32) for s in range(2)],
-                up_grouped[:].bitcast(F32).rearrange("p (s r u) -> p s r u", s=2, u=2),
+        def k_add(engine, b):
+            k_rotated = rotated_pool.tile([P, 2 * HEAD_DIM], F32, name="k_rotated", bufs=2)
+            add_planes(engine, k_products[b][:], k_rotated[:])
+            nc.sync.dma_start(
+                out=k_view[:, 2 * b : 2 * b + 2, :], in_=k_rotated[:].rearrange("p (s d) -> p s d", s=2)
             )
-            quantise(up_grouped[:], up_codes[:], up_scales[:])
 
-        def x_flip(i):
-            flip_block(x_raw[i][:], ("x", i))
+        def q_run(run):
+            q_passes(run, FIRST)
+            q_passes(run, SECOND)
+            q_product(run, FIRST)
+            q_add(nc.gpsimd, run, FIRST)
+            q_product(run, SECOND)
 
-        def x_quantise(i):
-            quantise_block(("x", i), x_codes[:, i], x_scales[:, i])
+        def keep_busy(count):
+            bank = sum_psum.tile([P, BUSY_COLS], F32, name="busy_sums", tag="sums")
+            for repeat in range(count):
+                nc.tensor.matmul(bank[:], lhsT=busy[:, 0:P], rhs=busy[:], start=True, stop=True)
 
-        def k_flip(t):
-            flip_block(wkv_raw[t][:], ("k", t))
-
-        def k_quantise(t):
-            quantise_block(("k", t), wkv_codes[:, t], wkv_scales[:, t])
-
-        x_flip(0)
-        x_quantise(0)
-        x_flip(1)
-        x_quantise(1)
+        keep_busy(6)
+        flip_x(0)
+        keep_busy(2)
+        flip_x(1)
+        keep_busy(2)
         flip_heads(0)
-        quantise_heads(0)
-        x_flip(2)
-        x_quantise(2)
-        x_flip(3)
-        x_quantise(3)
-        k_flip(0)
-        k_quantise(0)
-        k_flip(1)
-        k_quantise(1)
-        q_passes(0)
-        q_product(0, 0)
-        q_product(0, 1)
-        q_add(0, 0, nc.vector)
+        keep_busy(2)
+        flip_x(2)
+        keep_busy(2)
+        flip_x(3)
+        keep_busy(2)
+        flip_wkv(0)
+        keep_busy(2)
+        flip_wkv(1)
+        q_passes(0, FIRST)
+        q_product(0, FIRST)
+        q_add(nc.gpsimd, 0, FIRST)
         flip_heads(1)
-        quantise_heads(1)
-        q_add(0, 1, nc.vector)
-        k_flip(2)
-        k_quantise(2)
-        k_flip(3)
-        k_quantise(3)
-        up()
-        q_passes(1)
-        q_product(1, 0)
-        q_product(1, 1)
-        q_add(1, 0, nc.vector)
+        q_passes(0, SECOND)
+        q_product(0, SECOND)
+        flip_wkv(2)
+        q_add(nc.vector, 0, SECOND)
+        flip_wkv(3)
+        flip_up()
+        q_run(1)
         flip_heads(2)
-        quantise_heads(2)
-        q_add(1, 1, nc.vector)
-        latent(0)
+        q_add(nc.vector, 1, SECOND)
+        latent_passes(0)
         latent_quantise(0)
         flip_heads(3)
-        quantise_heads(3)
-        q_passes(2)
-        q_product(2, 0)
-        q_product(2, 1)
-        q_add(2, 0, nc.vector)
+        q_run(2)
         flip_heads(4)
-        quantise_heads(4)
-        q_add(2, 1, nc.vector)
-        latent(1)
+        q_add(nc.vector, 2, SECOND)
+        latent_passes(1)
         latent_quantise(1)
-        q_passes(3)
-        q_product(3, 0)
-        q_product(3, 1)
-        kv(0)
-        k_product(0)
-        q_add(3, 0, nc.vector)
+        q_run(3)
         flip_heads(5)
-        quantise_heads(5)
-        q_passes(4)
-        q_product(4, 0)
-        q_product(4, 1)
-        q_add(3, 1, nc.vector)
-        latent(2)
-        latent_quantise(2)
-        q_add(4, 0, nc.vector)
-        q_add(4, 1, nc.vector)
+        q_add(nc.vector, 3, SECOND)
+        kv_passes(0)
+        q_run(4)
+        k_product(0)
         flip_heads(6)
-        quantise_heads(6)
-        q_passes(5)
-        q_product(5, 0)
-        q_product(5, 1)
-        q_add(5, 0, nc.vector)
-        latent(3)
-        latent_quantise(3)
-        q_add(5, 1, nc.vector)
-        k_add(0, nc.vector)
+        q_add(nc.vector, 4, SECOND)
+        k_add(nc.vector, 0)
+        latent_passes(2)
+        latent_quantise(2)
+        q_run(5)
         flip_heads(7)
-        quantise_heads(7)
-        q_passes(6)
-        q_product(6, 0)
-        q_product(6, 1)
-        kv(1)
-        q_passes(7)
-        q_add(6, 0, nc.vector)
-        q_add(6, 1, nc.vector)
-        q_product(7, 0)
-        q_product(7, 1)
+        q_add(nc.vector, 5, SECOND)
+        latent_passes(3)
+        latent_quantise(3)
+        q_run(6)
+        kv_passes(1)
+        q_passes(7, FIRST)
+        q_passes(7, (2,))
+        q_passes(7, (3,))
+        q_add(nc.gpsimd, 6, SECOND)
         k_product(1)
-        q_add(7, 0, nc.vector)
-        q_add(7, 1, nc.vector)
-        k_add(1, nc.vector)
+        k_add(nc.gpsimd, 1)
+        q_product(7, FIRST)
+        q_add(nc.gpsimd, 7, FIRST)
+        q_product(7, (2,))
+        q_product(7, (3,))
+        q_add(nc.vector, 7, (2,))
+        q_add(nc.vector, 7, (3,))

@@ -27,6 +27,7 @@ RUNS = HEADS // RUN_HEADS
 RUN_COLS = RUN_HEADS * HEAD_DIM
 BUSY_COLS = 512
 FIRST, SECOND = (0, 1), (2, 3)
+GPSIMD_COLS = 320
 
 FLOPS = 2 * TOKENS * CHANNELS * (HEADS * HEAD_DIM + LATENT) + 2 * TOKENS * LATENT * 2 * HEAD_DIM
 
@@ -37,7 +38,7 @@ def tile_attention_pa_kernel(
     nc = tc.nc
     with ExitStack() as ctx:
         keep = ctx.enter_context(tc.tile_pool(name="keep", bufs=1))
-        block_pool = ctx.enter_context(tc.tile_pool(name="block_words", bufs=4))
+        block_pool = ctx.enter_context(tc.tile_pool(name="block_words", bufs=3))
         heads_pool = ctx.enter_context(tc.tile_pool(name="heads_words", bufs=3))
         wq_code_pool = ctx.enter_context(tc.tile_pool(name="wq_codes", bufs=4))
         product_pool = ctx.enter_context(tc.tile_pool(name="products", bufs=3))
@@ -58,6 +59,7 @@ def tile_attention_pa_kernel(
         x_raw = [keep.tile([P, CHANNELS], BF16, name="x_raw%d" % i) for i in range(TOKEN_BLOCKS)]
         wkv_raw = [keep.tile([P, CHANNELS], BF16, name="wkv_raw%d" % t) for t in range(LATENT_BLOCKS)]
         wq_raw = [keep.tile([P, RUN_HEADS, CHANNELS], BF16, name="wq_raw%d" % run) for run in range(RUNS)]
+        up_raw = [keep.tile([P, LATENT], BF16, name="up_raw%d" % s) for s in range(2)]
 
         def load_x(i):
             nc.sync.dma_start(out=x_raw[i][:], in_=x_blocks[i])
@@ -69,26 +71,28 @@ def tile_attention_pa_kernel(
             for channels in (slice(0, CHANNELS // 2), slice(CHANNELS // 2, CHANNELS)):
                 nc.sync.dma_start(out=wq_raw[run][:, :, channels], in_=wq_runs[run][:, :, channels])
 
+        def load_up():
+            for s, weight in enumerate((wk_up, wv_up)):
+                nc.sync.dma_start(out=up_raw[s][:], in_=weight)
+
         load_x(0)
-        load_x(1)
         load_heads(0)
+        load_x(1)
         load_x(2)
         load_x(3)
+        load_heads(1)
+        load_heads(2)
         load_wkv(0)
         load_wkv(1)
-        load_heads(1)
+        load_heads(3)
         load_wkv(2)
         load_wkv(3)
-        for run in range(2, RUNS):
+        load_up()
+        for run in range(4, RUNS):
             load_heads(run)
-        cos_raw = keep.tile([P, TOKEN_BLOCKS, PAIRS], BF16)
-        sin_raw = keep.tile([P, TOKEN_BLOCKS, PAIRS], BF16)
-        nc.scalar.dma_start(out=cos_raw[:], in_=cos_view)
-        nc.scalar.dma_start(out=sin_raw[:], in_=sin_view)
-        up_raw = []
-        for s, weight in enumerate((wk_up, wv_up)):
-            up_raw.append(keep.tile([P, LATENT], BF16, name="up_raw%d" % s))
-            nc.scalar.dma_start(out=up_raw[s][:], in_=weight)
+        angles = keep.tile([P, 4, TOKEN_BLOCKS, PAIRS], BF16)
+        for row, source in ((1, sin_view), (0, cos_view), (3, cos_view)):
+            nc.scalar.dma_start(out=angles[:, row], in_=source)
 
         busy = keep.tile([P, BUSY_COLS], BF16)
         nc.gpsimd.iota(
@@ -97,20 +101,18 @@ def tile_attention_pa_kernel(
         identity = keep.tile([P, P], F32)
         make_identity(nc, identity[:])
 
-        rotary = keep.tile([P, 2, 2, 2, RUN_HEADS, PAIRS, 2], BF16)
-        for e, o, source, sign in ((0, 0, cos_raw, 1.0), (0, 1, sin_raw, 1.0), (1, 0, sin_raw, -1.0), (1, 1, cos_raw, 1.0)):
-            nc.gpsimd.tensor_scalar(
-                out=rotary[:, :, e, :, 0, :, o],
-                in0=source[:].rearrange("p (b i) j -> p b i j", i=2),
-                scalar1=sign,
-                scalar2=0.0,
-                op0=MULT,
-                op1=ADD,
+        rotary = keep.tile([P, 2, TOKEN_BLOCKS, RUN_HEADS, PAIRS, 2], BF16)
+
+        def build_table():
+            nc.vector.tensor_scalar(out=angles[:, 2], in0=angles[:, 1], scalar1=-1.0, scalar2=0.0, op0=MULT, op1=ADD)
+            for e in range(2):
+                nc.vector.tensor_copy(
+                    out=rotary[:, e, :, 0], in_=angles[:, 2 * e : 2 * e + 2].rearrange("p o i j -> p i j o")
+                )
+            nc.vector.tensor_copy(
+                out=rotary[:, :, :, 1].rearrange("p e i j o -> p e i (j o)"),
+                in_=rotary[:, :, :, 0].rearrange("p e i j o -> p e i (j o)"),
             )
-        rotary_heads = rotary[:].rearrange("p b e i h j o -> p (b e i) h (j o)")
-        nc.gpsimd.tensor_scalar(
-            out=rotary_heads[:, :, 1], in0=rotary_heads[:, :, 0], scalar1=1.0, scalar2=0.0, op0=MULT, op1=ADD
-        )
 
         x_codes = keep.tile([P, TOKEN_BLOCKS, PASSES, P], U32, align_bytes=64)
         x_scales = keep.tile([P, TOKEN_BLOCKS, PASSES, P], U8, align_bytes=64)
@@ -137,13 +139,16 @@ def tile_attention_pa_kernel(
         def quantise(words, codes, scales):
             nc.vector.quantize_mx(out=codes.bitcast(FP8X4), scales=scales, in_=words)
 
-        def flip_block(raw, codes, scales):
+        def flip_block(raw):
             channels = raw.bitcast(F32).rearrange("p (g w) -> p g w", g=PASSES)
             words = block_pool.tile([P, PASSES, P * 4], BF16, name="block_words", align_bytes=64)
             for g in range(0, PASSES, 2):
                 flip_bank(
                     [channels[:, g], channels[:, g + 1]], words[:, g : g + 2].rearrange("p s w -> p (s w)")
                 )
+            return words
+
+        def quantise_block(words, codes, scales):
             for g in range(0, PASSES, 2):
                 quantise(
                     words[:, g : g + 2].rearrange("p s w -> p (s w)"),
@@ -151,11 +156,21 @@ def tile_attention_pa_kernel(
                     scales[:, g : g + 2].rearrange("p s r -> p (s r)"),
                 )
 
+        x_words = {}
+        wkv_words = {}
+        wq_words = {}
+
         def flip_x(i):
-            flip_block(x_raw[i][:], x_codes[:, i], x_scales[:, i])
+            x_words[i] = flip_block(x_raw[i][:])
+
+        def quantise_x(i):
+            quantise_block(x_words[i], x_codes[:, i], x_scales[:, i])
 
         def flip_wkv(t):
-            flip_block(wkv_raw[t][:], wkv_codes[:, t], wkv_scales[:, t])
+            wkv_words[t] = flip_block(wkv_raw[t][:])
+
+        def quantise_wkv(t):
+            quantise_block(wkv_words[t], wkv_codes[:, t], wkv_scales[:, t])
 
         def flip_heads(run):
             heads = [
@@ -164,15 +179,22 @@ def tile_attention_pa_kernel(
             words = heads_pool.tile([P, PASSES, RUN_COLS * 4], BF16, name="heads_words", align_bytes=64)
             for g in range(PASSES):
                 flip_bank([head[:, g] for head in heads], words[:, g])
+            wq_words[run] = words
+
+        def quantise_heads(run):
+            words = wq_words[run]
             wq_codes[run] = wq_code_pool.tile([P, PASSES, RUN_COLS], U32, name="run_codes", align_bytes=64)
             wq_scales[run] = wq_code_pool.tile([P, PASSES, RUN_COLS], U8, name="run_scales", align_bytes=64)
             for g in range(PASSES):
                 quantise(words[:, g], wq_codes[run][:, g, :], wq_scales[run][:, g, :])
 
+        up_words = keep.tile([P, 2 * HEAD_DIM * 4], BF16, align_bytes=64)
+
         def flip_up():
-            words = keep.tile([P, 2 * HEAD_DIM * 4], BF16, align_bytes=64)
-            flip_bank([up_raw[s][:].bitcast(F32) for s in range(2)], words[:])
-            quantise(words[:], up_codes[:], up_scales[:])
+            flip_bank([up_raw[s][:].bitcast(F32) for s in range(2)], up_words[:])
+
+        def quantise_up():
+            quantise(up_words[:], up_codes[:], up_scales[:])
 
         def form_products(sums, table, products):
             nc.vector.tensor_tensor(
@@ -184,6 +206,7 @@ def tile_attention_pa_kernel(
 
         q_sums = {}
         q_products = {}
+        q_rotated = {}
 
         def q_passes(run, blocks):
             bank = sum_psum.tile([P, len(blocks), RUN_COLS], F32, name="q_sums", tag="sums")
@@ -201,22 +224,26 @@ def tile_attention_pa_kernel(
             q_sums[run, blocks] = bank
 
         def q_product(run, blocks):
-            b, i = divmod(blocks[0], 2)
-            products = product_pool.tile([P, 2, len(blocks) * RUN_COLS], F32, name="q_products%d" % len(blocks), bufs=1 + len(blocks))
+            if run not in q_products:
+                q_products[run] = product_pool.tile([P, 2, TOKEN_BLOCKS * RUN_COLS], F32, name="q_products", bufs=2)
+            i, n = blocks[0], len(blocks)
             form_products(
                 q_sums[run, blocks][:].rearrange("p s (n e) -> p e (s n)", e=2),
-                rotary[:, b, :, i : i + len(blocks)].rearrange("p e i h j o -> p e (i h j) o"),
-                products[:].rearrange("p e (n o) -> p e n o", o=2),
+                rotary[:, :, i : i + n].rearrange("p e i h j o -> p e (i h j) o"),
+                q_products[run][:, :, i * RUN_COLS : (i + n) * RUN_COLS].rearrange("p e (n o) -> p e n o", o=2),
             )
-            q_products[run, blocks] = products
 
-        def q_add(engine, run, blocks):
-            rotated = rotated_pool.tile([P, len(blocks) * RUN_COLS], F32, name="q_rotated%d" % len(blocks), bufs=8 if blocks in (FIRST, SECOND) else 2)
-            add_planes(engine, q_products[run, blocks][:], rotated[:])
+        def q_add(engine, run, first, last):
+            if run not in q_rotated:
+                q_rotated[run] = rotated_pool.tile([P, TOKEN_BLOCKS * RUN_COLS], F32, name="q_rotated", bufs=5)
+            add_planes(engine, q_products[run][:, :, first:last], q_rotated[run][:, first:last])
+
+        def q_store(run, blocks):
+            i, n = blocks[0], len(blocks)
             heads = slice(run * RUN_HEADS, (run + 1) * RUN_HEADS)
             nc.sync.dma_start(
-                out=q_view[:, blocks[0] : blocks[-1] + 1, heads, :].rearrange("p i h d -> p i (h d)"),
-                in_=rotated[:].rearrange("p (i c) -> p i c", i=len(blocks)),
+                out=q_view[:, i : i + n, heads, :].rearrange("p i h d -> p i (h d)"),
+                in_=q_rotated[run][:, i * RUN_COLS : (i + n) * RUN_COLS].rearrange("p (i c) -> p i c", i=n),
             )
 
         def latent_passes(i):
@@ -269,7 +296,7 @@ def tile_attention_pa_kernel(
             k_products[b] = product_pool.tile([P, 2, 2 * HEAD_DIM], F32, name="k_products", bufs=2)
             form_products(
                 k_sums[b][:, 0].rearrange("p s (j e) -> p e s j", e=2),
-                rotary[:, b, :, :, 0],
+                rotary[:, :, 2 * b : 2 * b + 2, 0],
                 k_products[b][:].rearrange("p e (s j o) -> p e s j o", s=2, o=2),
             )
 
@@ -280,80 +307,109 @@ def tile_attention_pa_kernel(
                 out=k_view[:, 2 * b : 2 * b + 2, :], in_=k_rotated[:].rearrange("p (s d) -> p s d", s=2)
             )
 
-        def q_run(run):
-            q_passes(run, FIRST)
-            q_passes(run, SECOND)
-            q_product(run, FIRST)
-            q_add(nc.gpsimd, run, FIRST)
-            q_product(run, SECOND)
+        ALL = TOKEN_BLOCKS * RUN_COLS
 
         def keep_busy(count):
             bank = sum_psum.tile([P, BUSY_COLS], F32, name="busy_sums", tag="sums")
             for repeat in range(count):
                 nc.tensor.matmul(bank[:], lhsT=busy[:, 0:P], rhs=busy[:], start=True, stop=True)
 
-        keep_busy(6)
+        def heads(run):
+            flip_heads(run)
+            quantise_heads(run)
+
+        def wkv_pair(t):
+            for block in (t, t + 1):
+                flip_wkv(block)
+                quantise_wkv(block)
+
+        def q_pair(run):
+            q_product(run, FIRST)
+            q_add(nc.gpsimd, run, 0, GPSIMD_COLS)
+            q_product(run, SECOND)
+
+        def q_end(run):
+            q_add(nc.vector, run, GPSIMD_COLS, ALL)
+            q_store(run, FIRST + SECOND)
+
+        keep_busy(5)
         flip_x(0)
-        keep_busy(2)
+        quantise_x(0)
+        build_table()
+        keep_busy(1)
+        heads(0)
+        keep_busy(1)
         flip_x(1)
-        keep_busy(2)
-        flip_heads(0)
-        keep_busy(2)
+        quantise_x(1)
+        q_passes(0, (0,))
+        q_product(0, (0,))
         flip_x(2)
-        keep_busy(2)
+        quantise_x(2)
+        q_passes(0, (1,))
+        q_product(0, (1,))
+        q_add(nc.gpsimd, 0, 0, GPSIMD_COLS)
         flip_x(3)
-        keep_busy(2)
-        flip_wkv(0)
-        keep_busy(2)
-        flip_wkv(1)
-        q_passes(0, FIRST)
-        q_product(0, FIRST)
-        q_add(nc.gpsimd, 0, FIRST)
-        flip_heads(1)
+        quantise_x(3)
+        heads(1)
         q_passes(0, SECOND)
         q_product(0, SECOND)
-        flip_wkv(2)
-        q_add(nc.vector, 0, SECOND)
-        flip_wkv(3)
+        heads(2)
+        q_end(0)
+        q_passes(1, FIRST)
+        wkv_pair(0)
+        q_passes(1, SECOND)
+        q_pair(1)
+        heads(3)
+        q_end(1)
+        q_passes(2, FIRST)
+        wkv_pair(2)
         flip_up()
-        q_run(1)
-        flip_heads(2)
-        q_add(nc.vector, 1, SECOND)
+        quantise_up()
+        q_passes(2, SECOND)
+        q_pair(2)
+        heads(4)
+        q_end(2)
+        q_passes(3, FIRST)
+        heads(5)
+        q_passes(3, SECOND)
+        q_pair(3)
+        heads(6)
+        q_end(3)
         latent_passes(0)
-        latent_quantise(0)
-        flip_heads(3)
-        q_run(2)
-        flip_heads(4)
-        q_add(nc.vector, 2, SECOND)
+        heads(7)
         latent_passes(1)
+        latent_quantise(0)
         latent_quantise(1)
-        q_run(3)
-        flip_heads(5)
-        q_add(nc.vector, 3, SECOND)
-        kv_passes(0)
-        q_run(4)
-        k_product(0)
-        flip_heads(6)
-        q_add(nc.vector, 4, SECOND)
-        k_add(nc.vector, 0)
+        q_passes(4, FIRST)
+        q_passes(4, SECOND)
+        q_pair(4)
+        q_end(4)
         latent_passes(2)
         latent_quantise(2)
-        q_run(5)
-        flip_heads(7)
-        q_add(nc.vector, 5, SECOND)
+        q_passes(5, FIRST)
+        q_passes(5, SECOND)
+        q_pair(5)
+        q_end(5)
         latent_passes(3)
         latent_quantise(3)
-        q_run(6)
+        kv_passes(0)
+        q_passes(6, FIRST)
+        q_passes(6, SECOND)
+        q_pair(6)
+        k_product(0)
+        q_end(6)
         kv_passes(1)
         q_passes(7, FIRST)
         q_passes(7, (2,))
         q_passes(7, (3,))
-        q_add(nc.gpsimd, 6, SECOND)
+        k_add(nc.vector, 0)
         k_product(1)
         k_add(nc.gpsimd, 1)
         q_product(7, FIRST)
-        q_add(nc.gpsimd, 7, FIRST)
+        q_add(nc.gpsimd, 7, 0, GPSIMD_COLS)
         q_product(7, (2,))
         q_product(7, (3,))
-        q_add(nc.vector, 7, (2,))
-        q_add(nc.vector, 7, (3,))
+        q_add(nc.vector, 7, GPSIMD_COLS, 768)
+        q_store(7, (0, 1, 2))
+        q_add(nc.vector, 7, 768, ALL)
+        q_store(7, (3,))

@@ -27,7 +27,6 @@ RUNS = HEADS // RUN_HEADS
 RUN_COLS = RUN_HEADS * HEAD_DIM
 BUSY_COLS = 512
 FIRST, SECOND = (0, 1), (2, 3)
-GPSIMD_COLS = 320
 
 FLOPS = 2 * TOKENS * CHANNELS * (HEADS * HEAD_DIM + LATENT) + 2 * TOKENS * LATENT * 2 * HEAD_DIM
 
@@ -58,7 +57,10 @@ def tile_attention_pa_kernel(
 
         x_raw = [keep.tile([P, CHANNELS], BF16, name="x_raw%d" % i) for i in range(TOKEN_BLOCKS)]
         wkv_raw = [keep.tile([P, CHANNELS], BF16, name="wkv_raw%d" % t) for t in range(LATENT_BLOCKS)]
-        wq_raw = [keep.tile([P, RUN_HEADS, CHANNELS], BF16, name="wq_raw%d" % run) for run in range(RUNS)]
+        wq_raw = [
+            [keep.tile([P, RUN_HEADS, CHANNELS // 2], BF16, name="wq_raw%d_%d" % (run, half)) for half in range(2)]
+            for run in range(RUNS)
+        ]
         up_raw = [keep.tile([P, LATENT], BF16, name="up_raw%d" % s) for s in range(2)]
 
         def load_x(i):
@@ -68,8 +70,9 @@ def tile_attention_pa_kernel(
             nc.sync.dma_start(out=wkv_raw[t][:], in_=wkv_blocks[t // 2, t % 2])
 
         def load_heads(run):
-            for channels in (slice(0, CHANNELS // 2), slice(CHANNELS // 2, CHANNELS)):
-                nc.sync.dma_start(out=wq_raw[run][:, :, channels], in_=wq_runs[run][:, :, channels])
+            for half in range(2):
+                channels = slice(half * CHANNELS // 2, (half + 1) * CHANNELS // 2)
+                nc.sync.dma_start(out=wq_raw[run][half][:], in_=wq_runs[run][:, :, channels])
 
         def load_up():
             for s, weight in enumerate((wk_up, wv_up)):
@@ -173,12 +176,11 @@ def tile_attention_pa_kernel(
             quantise_block(wkv_words[t], wkv_codes[:, t], wkv_scales[:, t])
 
         def flip_heads(run):
-            heads = [
-                wq_raw[run][:, a, :].bitcast(F32).rearrange("p (g w) -> p g w", g=PASSES) for a in range(RUN_HEADS)
-            ]
             words = heads_pool.tile([P, PASSES, RUN_COLS * 4], BF16, name="heads_words", align_bytes=64)
             for g in range(PASSES):
-                flip_bank([head[:, g] for head in heads], words[:, g])
+                half, piece = divmod(g, PASSES // 2)
+                channels = slice(piece * K_PASS, (piece + 1) * K_PASS)
+                flip_bank([wq_raw[run][half][:, a, channels].bitcast(F32) for a in range(RUN_HEADS)], words[:, g])
             wq_words[run] = words
 
         def quantise_heads(run):
@@ -223,27 +225,33 @@ def tile_attention_pa_kernel(
                     )
             q_sums[run, blocks] = bank
 
+        def half_of(blocks):
+            return FIRST if blocks[0] in FIRST else SECOND
+
         def q_product(run, blocks):
-            if run not in q_products:
-                q_products[run] = product_pool.tile([P, 2, TOKEN_BLOCKS * RUN_COLS], F32, name="q_products", bufs=2)
+            half = half_of(blocks)
+            if (run, half) not in q_products:
+                q_products[run, half] = product_pool.tile([P, 2, 2, RUN_COLS], F32, name="q_products", bufs=3)
             i, n = blocks[0], len(blocks)
+            first = i - half[0]
             form_products(
-                q_sums[run, blocks][:].rearrange("p s (n e) -> p e (s n)", e=2),
-                rotary[:, :, i : i + n].rearrange("p e i h j o -> p e (i h j) o"),
-                q_products[run][:, :, i * RUN_COLS : (i + n) * RUN_COLS].rearrange("p e (n o) -> p e n o", o=2),
+                q_sums[run, blocks][:].rearrange("p s (n e) -> p e s n", e=2),
+                rotary[:, :, i : i + n].rearrange("p e i h j o -> p e i (h j) o"),
+                q_products[run, half][:, first : first + n].rearrange("p s e (n o) -> p e s n o", o=2),
             )
 
-        def q_add(engine, run, first, last):
-            if run not in q_rotated:
-                q_rotated[run] = rotated_pool.tile([P, TOKEN_BLOCKS * RUN_COLS], F32, name="q_rotated", bufs=5)
-            add_planes(engine, q_products[run][:, :, first:last], q_rotated[run][:, first:last])
-
-        def q_store(run, blocks):
+        def q_add(engine, run, blocks):
+            half = half_of(blocks)
+            if (run, half) not in q_rotated:
+                q_rotated[run, half] = rotated_pool.tile([P, 2, RUN_COLS], F32, name="q_rotated", bufs=8)
             i, n = blocks[0], len(blocks)
+            first = i - half[0]
+            products = q_products[run, half][:, first : first + n]
+            rotated = q_rotated[run, half][:, first : first + n]
+            engine.tensor_tensor(out=rotated, in0=products[:, :, 0], in1=products[:, :, 1], op=ADD)
             heads = slice(run * RUN_HEADS, (run + 1) * RUN_HEADS)
             nc.sync.dma_start(
-                out=q_view[:, i : i + n, heads, :].rearrange("p i h d -> p i (h d)"),
-                in_=q_rotated[run][:, i * RUN_COLS : (i + n) * RUN_COLS].rearrange("p (i c) -> p i c", i=n),
+                out=q_view[:, i : i + n, heads, :].rearrange("p i h d -> p i (h d)"), in_=rotated
             )
 
         def latent_passes(i):
@@ -307,8 +315,6 @@ def tile_attention_pa_kernel(
                 out=k_view[:, 2 * b : 2 * b + 2, :], in_=k_rotated[:].rearrange("p (s d) -> p s d", s=2)
             )
 
-        ALL = TOKEN_BLOCKS * RUN_COLS
-
         def keep_busy(count):
             bank = sum_psum.tile([P, BUSY_COLS], F32, name="busy_sums", tag="sums")
             for repeat in range(count):
@@ -325,12 +331,11 @@ def tile_attention_pa_kernel(
 
         def q_pair(run):
             q_product(run, FIRST)
-            q_add(nc.gpsimd, run, 0, GPSIMD_COLS)
+            q_add(nc.gpsimd, run, FIRST)
             q_product(run, SECOND)
 
         def q_end(run):
-            q_add(nc.vector, run, GPSIMD_COLS, ALL)
-            q_store(run, FIRST + SECOND)
+            q_add(nc.vector, run, SECOND)
 
         keep_busy(5)
         flip_x(0)
@@ -347,7 +352,7 @@ def tile_attention_pa_kernel(
         quantise_x(2)
         q_passes(0, (1,))
         q_product(0, (1,))
-        q_add(nc.gpsimd, 0, 0, GPSIMD_COLS)
+        q_add(nc.gpsimd, 0, FIRST)
         flip_x(3)
         quantise_x(3)
         heads(1)
@@ -406,10 +411,8 @@ def tile_attention_pa_kernel(
         k_product(1)
         k_add(nc.gpsimd, 1)
         q_product(7, FIRST)
-        q_add(nc.gpsimd, 7, 0, GPSIMD_COLS)
+        q_add(nc.gpsimd, 7, FIRST)
         q_product(7, (2,))
         q_product(7, (3,))
-        q_add(nc.vector, 7, GPSIMD_COLS, 768)
-        q_store(7, (0, 1, 2))
-        q_add(nc.vector, 7, 768, ALL)
-        q_store(7, (3,))
+        q_add(nc.vector, 7, (2,))
+        q_add(nc.vector, 7, (3,))

@@ -97,12 +97,10 @@ def tile_attention_pa_kernel(
         for row, source in ((1, sin_view), (0, cos_view), (3, cos_view)):
             nc.scalar.dma_start(out=angles[:, row], in_=source)
 
-        busy = keep.tile([P, BUSY_COLS], BF16)
-        nc.gpsimd.iota(
-            busy[:], pattern=[[7, BUSY_COLS]], base=-1792, channel_multiplier=5, allow_small_or_imprecise_dtypes=True
-        )
         identity = keep.tile([P, P], F32)
         make_identity(nc, identity[:])
+        busy = keep.tile([P, BUSY_COLS], BF16)
+        nc.vector.memset(busy[:], 1.0)
 
         rotary = keep.tile([P, 2, TOKEN_BLOCKS, RUN_HEADS, PAIRS, 2], BF16)
 
@@ -352,9 +350,9 @@ def tile_attention_pa_kernel(
         quantise_x(2)
         q_passes(0, (1,))
         q_product(0, (1,))
-        q_add(nc.gpsimd, 0, FIRST)
         flip_x(3)
         quantise_x(3)
+        q_add(nc.vector, 0, FIRST)
         heads(1)
         q_passes(0, SECOND)
         q_product(0, SECOND)
@@ -404,15 +402,18 @@ def tile_attention_pa_kernel(
         k_product(0)
         q_end(6)
         kv_passes(1)
-        q_passes(7, FIRST)
+        q_passes(7, (0,))
+        q_passes(7, (1,))
         q_passes(7, (2,))
         q_passes(7, (3,))
         k_add(nc.vector, 0)
         k_product(1)
+        q_product(7, (0,))
         k_add(nc.gpsimd, 1)
-        q_product(7, FIRST)
-        q_add(nc.gpsimd, 7, FIRST)
+        q_product(7, (1,))
+        q_add(nc.gpsimd, 7, (0,))
         q_product(7, (2,))
         q_product(7, (3,))
+        q_add(nc.vector, 7, (1,))
         q_add(nc.vector, 7, (2,))
         q_add(nc.vector, 7, (3,))

@@ -173,13 +173,16 @@ def tile_attention_pa_kernel(
         def quantise_wkv(t):
             quantise_block(wkv_words[t], wkv_codes[:, t], wkv_scales[:, t])
 
-        def flip_heads(run):
-            words = heads_pool.tile([P, PASSES, RUN_COLS * 4], BF16, name="heads_words", align_bytes=64)
-            for g in range(PASSES):
-                half, piece = divmod(g, PASSES // 2)
-                channels = slice(piece * K_PASS, (piece + 1) * K_PASS)
-                flip_bank([wq_raw[run][half][:, a, channels].bitcast(F32) for a in range(RUN_HEADS)], words[:, g])
-            wq_words[run] = words
+        def flip_heads(run, halves=(0, 1)):
+            if run not in wq_words:
+                wq_words[run] = heads_pool.tile([P, PASSES, RUN_COLS * 4], BF16, name="heads_words", align_bytes=64)
+            for half in halves:
+                for piece in range(PASSES // 2):
+                    channels = slice(piece * K_PASS, (piece + 1) * K_PASS)
+                    flip_bank(
+                        [wq_raw[run][half][:, a, channels].bitcast(F32) for a in range(RUN_HEADS)],
+                        wq_words[run][:, half * PASSES // 2 + piece],
+                    )
 
         def quantise_heads(run):
             words = wq_words[run]
@@ -229,7 +232,7 @@ def tile_attention_pa_kernel(
         def q_product(run, blocks):
             half = half_of(blocks)
             if (run, half) not in q_products:
-                q_products[run, half] = product_pool.tile([P, 2, 2, RUN_COLS], F32, name="q_products", bufs=3)
+                q_products[run, half] = product_pool.tile([P, 2, 2, RUN_COLS], F32, name="q_products", bufs=4)
             i, n = blocks[0], len(blocks)
             first = i - half[0]
             form_products(
@@ -332,16 +335,26 @@ def tile_attention_pa_kernel(
             q_add(nc.gpsimd, run, FIRST)
             q_product(run, SECOND)
 
+        def q_burst(run):
+            for half in (FIRST, SECOND):
+                q_product(run, half)
+                q_add(nc.gpsimd, run, half)
+            for half in (FIRST, SECOND):
+                q_product(run + 1, half)
+
         def q_end(run):
             q_add(nc.vector, run, SECOND)
 
-        keep_busy(5)
+        keep_busy(4)
         flip_x(0)
         quantise_x(0)
         build_table()
-        keep_busy(1)
-        heads(0)
-        keep_busy(1)
+        keep_busy(2)
+        flip_heads(0, (0,))
+        keep_busy(2)
+        flip_heads(0, (1,))
+        quantise_heads(0)
+        keep_busy(2)
         flip_x(1)
         quantise_x(1)
         q_passes(0, (0,))
@@ -385,35 +398,33 @@ def tile_attention_pa_kernel(
         latent_quantise(1)
         q_passes(4, FIRST)
         q_passes(4, SECOND)
-        q_pair(4)
-        q_end(4)
-        latent_passes(2)
-        latent_quantise(2)
         q_passes(5, FIRST)
         q_passes(5, SECOND)
-        q_pair(5)
-        q_end(5)
+        q_burst(4)
+        latent_passes(2)
         latent_passes(3)
+        q_add(nc.vector, 5, FIRST)
+        q_add(nc.vector, 5, SECOND)
+        latent_quantise(2)
         latent_quantise(3)
-        kv_passes(0)
         q_passes(6, FIRST)
         q_passes(6, SECOND)
+        kv_passes(0)
         q_pair(6)
         k_product(0)
-        q_end(6)
         kv_passes(1)
         q_passes(7, (0,))
         q_passes(7, (1,))
         q_passes(7, (2,))
         q_passes(7, (3,))
-        k_add(nc.vector, 0)
+        q_add(nc.gpsimd, 6, SECOND)
+        k_add(nc.gpsimd, 0)
         k_product(1)
         q_product(7, (0,))
         k_add(nc.gpsimd, 1)
         q_product(7, (1,))
-        q_add(nc.gpsimd, 7, (0,))
         q_product(7, (2,))
         q_product(7, (3,))
-        q_add(nc.vector, 7, (1,))
+        q_add(nc.vector, 7, FIRST)
         q_add(nc.vector, 7, (2,))
         q_add(nc.vector, 7, (3,))

from contextlib import ExitStack

import concourse.mybir as mybir
from concourse.masks import make_identity

F32 = mybir.dt.float32
BF16 = mybir.dt.bfloat16
U32 = mybir.dt.uint32
U8 = mybir.dt.uint8
FP8X4 = mybir.dt.float8_e4m3fn_x4
MULT = mybir.AluOpType.mult
ADD = mybir.AluOpType.add

P = 128
TOKENS = 512
CHANNELS = 2048
HEADS = 16
HEAD_DIM = 128
LATENT = 512
PAIRS = HEAD_DIM // 2
K_PASS = 512
PASSES = CHANNELS // K_PASS
TOKEN_BLOCKS = TOKENS // P
LATENT_BLOCKS = LATENT // P
RUN_HEADS = 2
RUNS = HEADS // RUN_HEADS
RUN_COLS = RUN_HEADS * HEAD_DIM
BUSY_COLS = 512
FIRST, SECOND = (0, 1), (2, 3)

FLOPS = 2 * TOKENS * CHANNELS * (HEADS * HEAD_DIM + LATENT) + 2 * TOKENS * LATENT * 2 * HEAD_DIM


def tile_attention_pa_kernel(
    tc, x, freqs_cos, freqs_sin, wq, wkv_down, wk_up, wv_up, out_0, out_1, out_2
):
    nc = tc.nc
    with ExitStack() as ctx:
        keep = ctx.enter_context(tc.tile_pool(name="keep", bufs=1))
        block_pool = ctx.enter_context(tc.tile_pool(name="block_words", bufs=3))
        heads_pool = ctx.enter_context(tc.tile_pool(name="heads_words", bufs=3))
        wq_code_pool = ctx.enter_context(tc.tile_pool(name="wq_codes", bufs=4))
        product_pool = ctx.enter_context(tc.tile_pool(name="products", bufs=3))
        rotated_pool = ctx.enter_context(tc.tile_pool(name="rotated", bufs=8))
        flip_psum = ctx.enter_context(tc.psum_pool(name="flips", bufs=4))
        sum_psum = ctx.enter_context(tc.psum_pool(name="sums", bufs=4))
        ctx.enter_context(tc.manual_schedule())

        x_blocks = x.flatten_outer_dims().rearrange("(p i) c -> i p c", i=TOKEN_BLOCKS)
        cos_view = freqs_cos.rearrange("(p i) j -> p i j", i=TOKEN_BLOCKS)
        sin_view = freqs_sin.rearrange("(p i) j -> p i j", i=TOKEN_BLOCKS)
        q_view = out_0.flatten_outer_dims().rearrange("(p i h) d -> p i h d", i=TOKEN_BLOCKS, h=HEADS)
        k_view = out_1.flatten_outer_dims().rearrange("(p i) d -> p i d", i=TOKEN_BLOCKS)
        v_view = out_2.flatten_outer_dims().rearrange("(p i) d -> p i d", i=TOKEN_BLOCKS)
        wkv_blocks = wkv_down.rearrange("(u p e) c -> u e p c", u=2, e=2)
        wq_runs = wq.rearrange("(n a p) c -> n p a c", a=RUN_HEADS, p=P)

        x_raw = [keep.tile([P, CHANNELS], BF16, name="x_raw%d" % i) for i in range(TOKEN_BLOCKS)]
        wkv_raw = [keep.tile([P, CHANNELS], BF16, name="wkv_raw%d" % t) for t in range(LATENT_BLOCKS)]
        wq_raw = [
            [keep.tile([P, RUN_HEADS, CHANNELS // 2], BF16, name="wq_raw%d_%d" % (run, half)) for half in range(2)]
            for run in range(RUNS)
        ]
        up_raw = [keep.tile([P, LATENT], BF16, name="up_raw%d" % s) for s in range(2)]

        def load_x(i):
            nc.sync.dma_start(out=x_raw[i][:], in_=x_blocks[i])

        def load_wkv(t):
            nc.sync.dma_start(out=wkv_raw[t][:], in_=wkv_blocks[t // 2, t % 2])

        def load_heads(run):
            for half in range(2):
                channels = slice(half * CHANNELS // 2, (half + 1) * CHANNELS // 2)
                nc.sync.dma_start(out=wq_raw[run][half][:], in_=wq_runs[run][:, :, channels])

        def load_up():
            for s, weight in enumerate((wk_up, wv_up)):
                nc.sync.dma_start(out=up_raw[s][:], in_=weight)

        load_x(0)
        load_heads(0)
        load_x(1)
        load_x(2)
        load_x(3)
        load_heads(1)
        load_heads(2)
        load_wkv(0)
        load_wkv(1)
        load_heads(3)
        load_wkv(2)
        load_wkv(3)
        load_up()
        for run in range(4, RUNS):
            load_heads(run)
        angles = keep.tile([P, 4, TOKEN_BLOCKS, PAIRS], BF16)
        for row, source in ((1, sin_view), (0, cos_view), (3, cos_view)):
            nc.scalar.dma_start(out=angles[:, row], in_=source)

        identity = keep.tile([P, P], F32)
        make_identity(nc, identity[:])
        busy = keep.tile([P, BUSY_COLS], BF16)
        nc.vector.memset(busy[:], 1.0)

        rotary = keep.tile([P, 2, TOKEN_BLOCKS, RUN_HEADS, PAIRS, 2], BF16)

        def build_table():
            nc.vector.tensor_scalar(out=angles[:, 2], in0=angles[:, 1], scalar1=-1.0, scalar2=0.0, op0=MULT, op1=ADD)
            for e in range(2):
                nc.vector.tensor_copy(
                    out=rotary[:, e, :, 0], in_=angles[:, 2 * e : 2 * e + 2].rearrange("p o i j -> p i j o")
                )
            nc.vector.tensor_copy(
                out=rotary[:, :, :, 1].rearrange("p e i j o -> p e i (j o)"),
                in_=rotary[:, :, :, 0].rearrange("p e i j o -> p e i (j o)"),
            )

        x_codes = keep.tile([P, TOKEN_BLOCKS, PASSES, P], U32, align_bytes=64)
        x_scales = keep.tile([P, TOKEN_BLOCKS, PASSES, P], U8, align_bytes=64)
        wkv_codes = keep.tile([P, LATENT_BLOCKS, PASSES, P], U32, align_bytes=64)
        wkv_scales = keep.tile([P, LATENT_BLOCKS, PASSES, P], U8, align_bytes=64)
        up_codes = keep.tile([P, 2 * HEAD_DIM], U32, align_bytes=64)
        up_scales = keep.tile([P, 2 * HEAD_DIM], U8, align_bytes=64)
        latent_words = keep.tile([P, TOKEN_BLOCKS, P * 4], BF16, align_bytes=64)
        latent_codes = keep.tile([P, TOKENS], U32, align_bytes=64)
        latent_scales = keep.tile([P, TOKENS], U8, align_bytes=64)
        wq_codes = {}
        wq_scales = {}

        def flip_bank(slabs, words):
            bank = flip_psum.tile([P, 2, 2, P], F32, name="bank")
            for s in range(2):
                for u in range(2):
                    nc.tensor.transpose(bank[:, s, u, :], slabs[s][:, u * P : (u + 1) * P], identity[:])
            nc.scalar.copy(
                out=words.bitcast(F32).rearrange("p (s r u) -> p s r u", s=2, u=2),
                in_=bank[:].rearrange("p s u r -> p s r u"),
            )

        def quantise(words, codes, scales):
            nc.vector.quantize_mx(out=codes.bitcast(FP8X4), scales=scales, in_=words)

        def flip_block(raw):
            channels = raw.bitcast(F32).rearrange("p (g w) -> p g w", g=PASSES)
            words = block_pool.tile([P, PASSES, P * 4], BF16, name="block_words", align_bytes=64)
            for g in range(0, PASSES, 2):
                flip_bank(
                    [channels[:, g], channels[:, g + 1]], words[:, g : g + 2].rearrange("p s w -> p (s w)")
                )
            return words

        def quantise_block(words, codes, scales):
            for g in range(0, PASSES, 2):
                quantise(
                    words[:, g : g + 2].rearrange("p s w -> p (s w)"),
                    codes[:, g : g + 2].rearrange("p s r -> p (s r)"),
                    scales[:, g : g + 2].rearrange("p s r -> p (s r)"),
                )

        x_words = {}
        wkv_words = {}
        wq_words = {}

        def flip_x(i):
            x_words[i] = flip_block(x_raw[i][:])

        def quantise_x(i):
            quantise_block(x_words[i], x_codes[:, i], x_scales[:, i])

        def flip_wkv(t):
            wkv_words[t] = flip_block(wkv_raw[t][:])

        def quantise_wkv(t):
            quantise_block(wkv_words[t], wkv_codes[:, t], wkv_scales[:, t])

        def flip_heads(run, halves=(0, 1)):
            if run not in wq_words:
                wq_words[run] = heads_pool.tile([P, PASSES, RUN_COLS * 4], BF16, name="heads_words", align_bytes=64)
            for half in halves:
                for piece in range(PASSES // 2):
                    channels = slice(piece * K_PASS, (piece + 1) * K_PASS)
                    flip_bank(
                        [wq_raw[run][half][:, a, channels].bitcast(F32) for a in range(RUN_HEADS)],
                        wq_words[run][:, half * PASSES // 2 + piece],
                    )

        def quantise_heads(run):
            words = wq_words[run]
            wq_codes[run] = wq_code_pool.tile([P, PASSES, RUN_COLS], U32, name="run_codes", align_bytes=64)
            wq_scales[run] = wq_code_pool.tile([P, PASSES, RUN_COLS], U8, name="run_scales", align_bytes=64)
            for g in range(PASSES):
                quantise(words[:, g], wq_codes[run][:, g, :], wq_scales[run][:, g, :])

        up_words = keep.tile([P, 2 * HEAD_DIM * 4], BF16, align_bytes=64)

        def flip_up():
            flip_bank([up_raw[s][:].bitcast(F32) for s in range(2)], up_words[:])

        def quantise_up():
            quantise(up_words[:], up_codes[:], up_scales[:])

        def form_products(sums, table, products):
            nc.vector.tensor_tensor(
                out=products, in0=sums.unsqueeze(len(table.shape) - 1).to_broadcast(table.shape), in1=table, op=MULT
            )

        def add_planes(engine, products, rotated):
            engine.tensor_tensor(out=rotated, in0=products[:, 0], in1=products[:, 1], op=ADD)

        q_sums = {}
        q_products = {}
        q_rotated = {}

        def q_passes(run, blocks):
            bank = sum_psum.tile([P, len(blocks), RUN_COLS], F32, name="q_sums", tag="sums")
            for s, i in enumerate(blocks):
                for g in range(PASSES):
                    nc.tensor.matmul_mx(
                        out=bank[:, s, :],
                        lhsT=x_codes[:, i, g, :].bitcast(FP8X4),
                        lhsT_scale=x_scales[:, i, g, :],
                        rhs=wq_codes[run][:, g, :].bitcast(FP8X4),
                        rhs_scale=wq_scales[run][:, g, :],
                        start=(g == 0),
                        stop=(g == PASSES - 1),
                    )
            q_sums[run, blocks] = bank

        def half_of(blocks):
            return FIRST if blocks[0] in FIRST else SECOND

        def q_product(run, blocks):
            half = half_of(blocks)
            if (run, half) not in q_products:
                q_products[run, half] = product_pool.tile([P, 2, 2, RUN_COLS], F32, name="q_products", bufs=4)
            i, n = blocks[0], len(blocks)
            first = i - half[0]
            form_products(
                q_sums[run, blocks][:].rearrange("p s (n e) -> p e s n", e=2),
                rotary[:, :, i : i + n].rearrange("p e i h j o -> p e i (h j) o"),
                q_products[run, half][:, first : first + n].rearrange("p s e (n o) -> p e s n o", o=2),
            )

        def q_add(engine, run, blocks):
            half = half_of(blocks)
            if (run, half) not in q_rotated:
                q_rotated[run, half] = rotated_pool.tile([P, 2, RUN_COLS], F32, name="q_rotated", bufs=8)
            i, n = blocks[0], len(blocks)
            first = i - half[0]
            products = q_products[run, half][:, first : first + n]
            rotated = q_rotated[run, half][:, first : first + n]
            engine.tensor_tensor(out=rotated, in0=products[:, :, 0], in1=products[:, :, 1], op=ADD)
            heads = slice(run * RUN_HEADS, (run + 1) * RUN_HEADS)
            nc.sync.dma_start(
                out=q_view[:, i : i + n, heads, :].rearrange("p i h d -> p i (h d)"), in_=rotated
            )

        def latent_passes(i):
            bank = sum_psum.tile([P, LATENT_BLOCKS, P], F32, name="latent_sums", tag="sums")
            for t in range(LATENT_BLOCKS):
                for g in range(PASSES):
                    nc.tensor.matmul_mx(
                        out=bank[:, t, :],
                        lhsT=wkv_codes[:, t, g, :].bitcast(FP8X4),
                        lhsT_scale=wkv_scales[:, t, g, :],
                        rhs=x_codes[:, i, g, :].bitcast(FP8X4),
                        rhs_scale=x_scales[:, i, g, :],
                        start=(g == 0),
                        stop=(g == PASSES - 1),
                    )
            nc.scalar.copy(
                out=latent_words[:, i].rearrange("p (r t) -> p r t", t=LATENT_BLOCKS),
                in_=bank[:].rearrange("p t r -> p r t"),
            )

        def latent_quantise(i):
            tokens = slice(i * P, (i + 1) * P)
            quantise(latent_words[:, i], latent_codes[:, tokens], latent_scales[:, tokens])

        k_sums = {}

        def kv_passes(b):
            bank = sum_psum.tile([P, 2, 2, HEAD_DIM], F32, name="kv_sums", tag="sums")
            for w in range(2):
                columns = slice(w * HEAD_DIM, (w + 1) * HEAD_DIM)
                for s in range(2):
                    tokens = slice((2 * b + s) * P, (2 * b + s + 1) * P)
                    nc.tensor.matmul_mx(
                        out=bank[:, w, s, :],
                        lhsT=latent_codes[:, tokens].bitcast(FP8X4),
                        lhsT_scale=latent_scales[:, tokens],
                        rhs=up_codes[:, columns].bitcast(FP8X4),
                        rhs_scale=up_scales[:, columns],
                        start=True,
                        stop=True,
                    )
            v_copied = rotated_pool.tile([P, 2, HEAD_DIM], F32, name="v_copied", bufs=2)
            nc.scalar.copy(out=v_copied[:], in_=bank[:, 1])
            nc.sync.dma_start(out=v_view[:, 2 * b : 2 * b + 2, :], in_=v_copied[:])
            k_sums[b] = bank

        k_products = {}

        def k_product(b):
            k_products[b] = product_pool.tile([P, 2, 2 * HEAD_DIM], F32, name="k_products", bufs=2)
            form_products(
                k_sums[b][:, 0].rearrange("p s (j e) -> p e s j", e=2),
                rotary[:, :, 2 * b : 2 * b + 2, 0],
                k_products[b][:].rearrange("p e (s j o) -> p e s j o", s=2, o=2),
            )

        def k_add(engine, b):
            k_rotated = rotated_pool.tile([P, 2 * HEAD_DIM], F32, name="k_rotated", bufs=2)
            add_planes(engine, k_products[b][:], k_rotated[:])
            nc.sync.dma_start(
                out=k_view[:, 2 * b : 2 * b + 2, :], in_=k_rotated[:].rearrange("p (s d) -> p s d", s=2)
            )

        def keep_busy(count):
            bank = sum_psum.tile([P, BUSY_COLS], F32, name="busy_sums", tag="sums")
            for repeat in range(count):
                nc.tensor.matmul(bank[:], lhsT=busy[:, 0:P], rhs=busy[:], start=True, stop=True)

        def heads(run):
            flip_heads(run)
            quantise_heads(run)

        def wkv_pair(t):
            for block in (t, t + 1):
                flip_wkv(block)
                quantise_wkv(block)

        def q_pair(run):
            q_product(run, FIRST)
            q_add(nc.gpsimd, run, FIRST)
            q_product(run, SECOND)

        def q_burst(run):
            for half in (FIRST, SECOND):
                q_product(run, half)
                q_add(nc.gpsimd, run, half)
            for half in (FIRST, SECOND):
                q_product(run + 1, half)

        def q_end(run):
            q_add(nc.vector, run, SECOND)

        keep_busy(4)
        flip_x(0)
        quantise_x(0)
        build_table()
        keep_busy(2)
        flip_heads(0, (0,))
        keep_busy(2)
        flip_heads(0, (1,))
        quantise_heads(0)
        keep_busy(2)
        flip_x(1)
        quantise_x(1)
        q_passes(0, (0,))
        q_product(0, (0,))
        flip_x(2)
        quantise_x(2)
        q_passes(0, (1,))
        q_product(0, (1,))
        flip_x(3)
        quantise_x(3)
        q_add(nc.vector, 0, FIRST)
        heads(1)
        q_passes(0, SECOND)
        q_product(0, SECOND)
        heads(2)
        q_end(0)
        q_passes(1, FIRST)
        wkv_pair(0)
        q_passes(1, SECOND)
        q_pair(1)
        heads(3)
        q_end(1)
        q_passes(2, FIRST)
        wkv_pair(2)
        flip_up()
        quantise_up()
        q_passes(2, SECOND)
        q_pair(2)
        heads(4)
        q_end(2)
        q_passes(3, FIRST)
        heads(5)
        q_passes(3, SECOND)
        q_pair(3)
        heads(6)
        q_end(3)
        latent_passes(0)
        heads(7)
        latent_passes(1)
        latent_quantise(0)
        latent_quantise(1)
        q_passes(4, FIRST)
        q_passes(4, SECOND)
        q_passes(5, FIRST)
        q_passes(5, SECOND)
        q_burst(4)
        latent_passes(2)
        latent_passes(3)
        q_add(nc.vector, 5, FIRST)
        q_add(nc.vector, 5, SECOND)
        latent_quantise(2)
        latent_quantise(3)
        q_passes(6, FIRST)
        q_passes(6, SECOND)
        kv_passes(0)
        q_pair(6)
        k_product(0)
        kv_passes(1)
        q_passes(7, (0,))
        q_passes(7, (1,))
        q_passes(7, (2,))
        q_passes(7, (3,))
        q_add(nc.gpsimd, 6, SECOND)
        k_add(nc.gpsimd, 0)
        k_product(1)
        q_product(7, (0,))
        k_add(nc.gpsimd, 1)
        q_product(7, (1,))
        q_product(7, (2,))
        q_product(7, (3,))
        q_add(nc.vector, 7, FIRST)
        q_add(nc.vector, 7, (2,))
        q_add(nc.vector, 7, (3,))
